import numpy as np
import ml_dtypes


def mxq(x, axis, fmt="e4m3"):
    dtype, down = {"e4m3": (ml_dtypes.float8_e4m3fn, 7), "e5m2": (ml_dtypes.float8_e5m2, 14)}[fmt]
    v = np.moveaxis(np.asarray(x, np.float32).astype(ml_dtypes.bfloat16).astype(np.float64), axis, -1)
    blocks = v.reshape(v.shape[:-1] + (-1, 32))
    amax = np.abs(blocks).max(-1, keepdims=True)
    byte = np.maximum(np.where(amax > 0, np.frexp(amax)[1] - 1 + 127, 0) - down, 1)
    scale = np.exp2(byte - 127.0)
    codes = (blocks / scale).astype(np.float32).astype(dtype).astype(np.float64)
    return np.moveaxis((codes * scale).reshape(v.shape), -1, axis)


WIDE = False


def mx_kscale(k):
    if not WIDE:
        return np.ones(k)
    levels = np.array([10, -10, 5, -5, 0])
    a = np.random.permutation(np.resize(levels, k // 512 * 4)).reshape(k // 512, 4)
    idx = np.arange(k)
    return np.exp2(a[idx // 512, idx % 128 // 32])


BF16 = ml_dtypes.bfloat16


def bf(x):
    return np.asarray(x, np.float32).astype(BF16)


def f64(x):
    return np.asarray(x).astype(np.float64)


N, E, DIM = 16384, 512, 512
DENSITY = 0.005
BARE = 0.02


def draw_incidence():
    inc = np.random.random((N, E)) < DENSITY
    inc[np.random.random(N) < BARE, :] = False
    inc[:, np.random.random(E) < BARE] = False
    return bf(inc)


def setup_inputs():
    t = mx_kscale(DIM)
    return {
        "x_0_local": bf(np.random.standard_normal((N, DIM)) * t),
        "x_1_new": bf(np.random.standard_normal((E, DIM)) * 1.3),
        "incidence_1": draw_incidence(),
        "Wr": bf(np.random.standard_normal((DIM, DIM)) * 2.0 / np.sqrt(DIM) / t[:, None]),
        "br": bf(np.random.standard_normal(DIM) * 0.3),
        "gate_return": bf(0.8 + 0.4 * np.random.random(1)),
    }


def reference(x_0_local, x_1_new, incidence_1, Wr, br, gate_return):
    H = f64(incidence_1)
    D_v = np.maximum(H.sum(1, keepdims=True), 1.0)
    D_e = np.maximum(H.sum(0, keepdims=True), 1.0)
    H_norm = H / np.sqrt(D_v) / np.sqrt(D_e)
    ret_msg = mxq(H_norm.T, 1, "e4m3") @ mxq(f64(x_0_local), 0, "e4m3")
    upd = (mxq(ret_msg, 1, "e4m3") @ mxq(f64(Wr), 0, "e4m3")) + f64(br)
    return f64(x_1_new) + np.tanh(f64(gate_return)) * upd

@@ -1,0 +1,218 @@
+from contextlib import ExitStack
+
+import concourse.mybir as mybir
+from concourse.masks import make_identity
+
+BF16 = mybir.dt.bfloat16
+F32 = mybir.dt.float32
+U32 = mybir.dt.uint32
+U8 = mybir.dt.uint8
+FP8X4 = mybir.dt.float8_e4m3fn_x4
+MULT = mybir.AluOpType.mult
+ADD = mybir.AluOpType.add
+ACT = mybir.ActivationFunctionType
+
+NODES, EDGES, DIM = 16384, 512, 512
+P = 128
+PACK = 4
+K_PASS = P * PACK
+PASSES = NODES // K_PASS
+TILES = 4
+CHUNK = 2
+ROWS_ON_VECTOR = 3
+A_BATCH = 8
+ONES_COLS = 32
+RUN = 4
+X_COLS_ON_VECTOR = 192
+
+FLOPS = 2 * NODES * EDGES * DIM + 2 * EDGES * DIM * DIM
+
+
+def regroup(copy, grouped, rows, cols):
+    copy(
+        out=grouped[:, cols, :].rearrange("p (c i) t -> p c t i", i=RUN),
+        in_=rows[:, :, cols].rearrange("p t (c i) -> p c t i", i=RUN),
+    )
+
+
+def quantise(nc, codes, scales, grouped):
+    nc.vector.quantize_mx(
+        out=codes[:].bitcast(FP8X4),
+        scales=scales[:],
+        in_=grouped[:].rearrange("p w t -> p (w t)"),
+    )
+
+
+def tile_hypergraphgpslayer_pb_k_kernel(
+    tc, x_0_local, x_1_new, incidence_1, Wr, br, gate_return, out
+):
+    nc = tc.nc
+    h_view = incidence_1.rearrange("(c p t) e -> p c t e", p=P, t=PACK)
+    x_view = x_0_local.rearrange("(c p t) d -> p c t d", p=P, t=PACK)
+
+    with ExitStack() as stack:
+        keep = stack.enter_context(tc.tile_pool(name="keep", bufs=1))
+        work = stack.enter_context(tc.tile_pool(name="work", bufs=3))
+        psum = stack.enter_context(tc.psum_pool(name="psum", bufs=1))
+
+        def packed_tiles(pool, tag):
+            codes = pool.tile([P, 512], U32, name=tag + "_codes", tag=tag + "_codes", align_bytes=64)
+            scales = pool.tile([P, 512], U8, name=tag + "_scales", tag=tag + "_scales", align_bytes=64)
+            return codes, scales
+
+        gate_raw = keep.tile([P, 1], BF16)
+        nc.sync.dma_start(out=gate_raw[:], in_=gate_return.partition_broadcast(P))
+        gate = keep.tile([P, 1], F32)
+        nc.scalar.activation(out=gate[:], in_=gate_raw[:], func=ACT.Tanh)
+        ones = keep.tile([P, ONES_COLS], BF16)
+        nc.vector.memset(ones[:], 1.0)
+        ident = keep.tile([P, P], F32)
+        make_identity(nc, ident[:])
+
+        sum_v = keep.tile([P, PASSES, ROWS_ON_VECTOR], F32)
+        sum_s = keep.tile([P, PASSES, PACK - ROWS_ON_VECTOR], F32)
+        deg_v = keep.tile([P, PASSES, PACK], F32)
+        root_v = keep.tile([P, PASSES, PACK], F32)
+        a = keep.tile([P, PASSES, PACK], F32)
+        col_ps = [psum.tile([P, ONES_COLS], F32, name="col%d" % j, tag="acc%d" % j) for j in range(TILES)]
+        h_tiles = []
+        for k in range(PASSES // CHUNK):
+            h_tile = keep.tile([P, CHUNK, PACK, EDGES], BF16, name="h%d" % k)
+            nc.sync.dma_start(out=h_tile[:], in_=h_view[:, k * CHUNK : (k + 1) * CHUNK])
+            h_tiles.append(h_tile)
+            for cc in range(CHUNK):
+                c = k * CHUNK + cc
+                for t in range(PACK):
+                    row = h_tile[:, cc, t, :]
+                    if t < ROWS_ON_VECTOR:
+                        unread_v = work.tile([P, EDGES], BF16, tag="unread_v", bufs=4)
+                        nc.vector.tensor_scalar(
+                            out=unread_v[:], in0=row, scalar1=1.0, scalar2=None,
+                            op0=MULT, op1=ADD, accum_out=sum_v[:, c, t : t + 1],
+                        )
+                    else:
+                        unread_s = work.tile([P, EDGES], BF16, tag="unread_s", bufs=2)
+                        nc.scalar.activation(
+                            out=unread_s[:], in_=row, func=ACT.Copy,
+                            accum_out=sum_s[:, c, t - ROWS_ON_VECTOR : t - ROWS_ON_VECTOR + 1],
+                        )
+                    for j in range(TILES):
+                        nc.tensor.matmul(
+                            out=col_ps[j][:],
+                            lhsT=h_tile[:, cc, t, j * P : (j + 1) * P],
+                            rhs=ones[:],
+                            start=(c == 0 and t == 0),
+                            stop=(c == PASSES - 1 and t == PACK - 1),
+                        )
+                if (c + 1) % A_BATCH == 0:
+                    batch = slice(c + 1 - A_BATCH, c + 1)
+                    nc.vector.tensor_scalar_max(
+                        out=deg_v[:, batch, :ROWS_ON_VECTOR], in0=sum_v[:, batch, :], scalar1=1.0
+                    )
+                    nc.vector.tensor_scalar_max(
+                        out=deg_v[:, batch, ROWS_ON_VECTOR:], in0=sum_s[:, batch, :], scalar1=1.0
+                    )
+                    nc.scalar.activation(out=root_v[:, batch, :], in_=deg_v[:, batch, :], func=ACT.Sqrt)
+                    nc.vector.reciprocal(out=a[:, batch, :], in_=root_v[:, batch, :])
+
+        deg_e = keep.tile([P, TILES], F32)
+        root_e = keep.tile([P, TILES], F32)
+        b_col = keep.tile([P, TILES], F32)
+        for j in range(TILES):
+            nc.vector.tensor_scalar_max(out=deg_e[:, j : j + 1], in0=col_ps[j][:, 0:1], scalar1=1.0)
+        nc.scalar.activation(out=root_e[:], in_=deg_e[:], func=ACT.Sqrt)
+        nc.vector.reciprocal(out=b_col[:], in_=root_e[:])
+        b_ps = psum.tile([P, EDGES], F32, tag="spread")
+        for j in range(TILES):
+            nc.tensor.matmul(
+                out=b_ps[:, j * P : (j + 1) * P],
+                lhsT=b_col[:, j : j + 1].to_broadcast([P, P]),
+                rhs=ident[:],
+                start=True,
+                stop=True,
+            )
+
+        w_rows = work.tile([P, PACK, DIM], BF16, tag="x_rows", bufs=4)
+        nc.sync.dma_start(out=w_rows[:], in_=Wr.rearrange("(t p) n -> p t n", p=P))
+        w_grouped = work.tile([P, DIM, PACK], BF16, tag="x_grouped", align_bytes=64)
+        regroup(nc.scalar.copy, w_grouped, w_rows, slice(0, DIM))
+        w_codes, w_scales = packed_tiles(keep, "w")
+        quantise(nc, w_codes, w_scales, w_grouped)
+
+        x1_rows = work.tile([P, TILES, DIM], BF16, tag="x_rows", bufs=4)
+        nc.sync.dma_start(out=x1_rows[:], in_=x_1_new.rearrange("(i p) d -> p i d", p=P))
+        br_all = keep.tile([P, DIM], BF16)
+        nc.sync.dma_start(out=br_all[:], in_=br.partition_broadcast(P))
+        rest = keep.tile([P, TILES, DIM], F32)
+        for i in range(TILES):
+            nc.vector.scalar_tensor_tensor(
+                out=rest[:, i, :], in0=br_all[:], scalar=gate[:, 0:1], in1=x1_rows[:, i, :],
+                op0=MULT, op1=ADD,
+            )
+
+        ret_ps = [psum.tile([P, EDGES], F32, name="ret%d" % j, tag="acc%d" % j) for j in range(TILES)]
+        grouped_of = {}
+
+        def prepare(c):
+            x_rows = work.tile([P, PACK, DIM], BF16, tag="x_rows", bufs=4)
+            nc.sync.dma_start(out=x_rows[:], in_=x_view[:, c])
+            x_grouped = work.tile([P, DIM, PACK], BF16, tag="x_grouped", align_bytes=64)
+            regroup(nc.vector.tensor_copy, x_grouped, x_rows, slice(0, X_COLS_ON_VECTOR))
+            regroup(nc.scalar.copy, x_grouped, x_rows, slice(X_COLS_ON_VECTOR, DIM))
+            h_norm = work.tile([P, PACK, EDGES], BF16, tag="h_norm")
+            for t in range(PACK):
+                nc.vector.scalar_tensor_tensor(
+                    out=h_norm[:, t, :], in0=h_tiles[c // CHUNK][:, c % CHUNK, t, :],
+                    scalar=a[:, c, t : t + 1], in1=b_ps[:], op0=MULT, op1=MULT,
+                )
+            h_grouped = work.tile([P, EDGES, PACK], BF16, tag="h_grouped", align_bytes=64)
+            regroup(nc.scalar.copy, h_grouped, h_norm, slice(0, EDGES))
+            grouped_of[c] = (x_grouped, h_grouped)
+
+        def multiply(c):
+            x_grouped, h_grouped = grouped_of[c]
+            x_codes, x_scales = packed_tiles(work, "x")
+            quantise(nc, x_codes, x_scales, x_grouped)
+            h_codes, h_scales = packed_tiles(work, "h")
+            quantise(nc, h_codes, h_scales, h_grouped)
+            for j in range(TILES):
+                cols = slice(j * P, (j + 1) * P)
+                nc.tensor.matmul_mx(
+                    out=ret_ps[j][:],
+                    lhsT=x_codes[:, cols].bitcast(FP8X4), lhsT_scale=x_scales[:, cols],
+                    rhs=h_codes[:].bitcast(FP8X4), rhs_scale=h_scales[:],
+                    start=(c == 0), stop=(c == PASSES - 1),
+                )
+
+        prepare(0)
+        for c in range(1, PASSES):
+            prepare(c)
+            multiply(c - 1)
+        multiply(PASSES - 1)
+
+        r_rows = work.tile([P, PACK, EDGES], BF16, tag="h_norm")
+        for j in range(TILES):
+            if j % 2 == 0:
+                nc.vector.tensor_copy(out=r_rows[:, j, :], in_=ret_ps[j][:])
+            else:
+                nc.scalar.copy(out=r_rows[:, j, :], in_=ret_ps[j][:])
+        r_grouped = work.tile([P, EDGES, PACK], BF16, tag="h_grouped", align_bytes=64)
+        regroup(nc.vector.tensor_copy, r_grouped, r_rows, slice(0, EDGES))
+        r_codes, r_scales = packed_tiles(work, "h")
+        quantise(nc, r_codes, r_scales, r_grouped)
+
+        for i in range(TILES):
+            cols = slice(i * P, (i + 1) * P)
+            upd_ps = psum.tile([P, DIM], F32, name="upd%d" % i, tag="acc%d" % i)
+            nc.tensor.matmul_mx(
+                out=upd_ps[:],
+                lhsT=r_codes[:, cols].bitcast(FP8X4), lhsT_scale=r_scales[:, cols],
+                rhs=w_codes[:].bitcast(FP8X4), rhs_scale=w_scales[:],
+                start=True, stop=True,
+            )
+            result = work.tile([P, DIM], F32, tag="x_rows", bufs=4)
+            nc.vector.scalar_tensor_tensor(
+                out=result[:], in0=upd_ps[:], scalar=gate[:, 0:1], in1=rest[:, i, :],
+                op0=MULT, op1=ADD,
+            )
+            nc.sync.dma_start(out=out[cols, :], in_=result[:])

@@ -18,21 +18,22 @@ PACK = 4
 K_PASS = P * PACK
 PASSES = NODES // K_PASS
 TILES = 4
-CHUNK = 2
-ROWS_ON_VECTOR = 3
+ROWS_ON_VECTOR = 2
 A_BATCH = 8
 ONES_COLS = 32
 RUN = 4
-X_COLS_ON_VECTOR = 192
+X_COLS_ON_GPSIMD = 320
+X_AHEAD = 4
 
 FLOPS = 2 * NODES * EDGES * DIM + 2 * EDGES * DIM * DIM
 
 
-def regroup(copy, grouped, rows, cols):
-    copy(
-        out=grouped[:, cols, :].rearrange("p (c i) t -> p c t i", i=RUN),
-        in_=rows[:, :, cols].rearrange("p t (c i) -> p c t i", i=RUN),
-    )
+def by_column(grouped, cols):
+    return grouped[:, cols, :].rearrange("p (c i) t -> p c t i", i=RUN)
+
+
+def by_row(rows, cols):
+    return rows[:, :, cols].rearrange("p t (c i) -> p c t i", i=RUN)
 
 
 def quantise(nc, codes, scales, grouped):
@@ -49,11 +50,18 @@ def tile_hypergraphgpslayer_pb_k_kernel(
     nc = tc.nc
     h_view = incidence_1.rearrange("(c p t) e -> p c t e", p=P, t=PACK)
     x_view = x_0_local.rearrange("(c p t) d -> p c t d", p=P, t=PACK)
+    all_cols = slice(0, 512)
 
     with ExitStack() as stack:
         keep = stack.enter_context(tc.tile_pool(name="keep", bufs=1))
-        work = stack.enter_context(tc.tile_pool(name="work", bufs=3))
+        work = stack.enter_context(tc.tile_pool(name="work", bufs=2))
         psum = stack.enter_context(tc.psum_pool(name="psum", bufs=1))
+
+        def rows_tile(tag, bufs):
+            return work.tile([P, PACK, 512], BF16, name=tag, tag=tag, bufs=bufs)
+
+        def grouped_tile(tag):
+            return work.tile([P, 512, PACK], BF16, name=tag, tag=tag, align_bytes=64)
 
         def packed_tiles(pool, tag):
             codes = pool.tile([P, 512], U32, name=tag + "_codes", tag=tag + "_codes", align_bytes=64)
@@ -76,44 +84,41 @@ def tile_hypergraphgpslayer_pb_k_kernel(
         a = keep.tile([P, PASSES, PACK], F32)
         col_ps = [psum.tile([P, ONES_COLS], F32, name="col%d" % j, tag="acc%d" % j) for j in range(TILES)]
         h_tiles = []
-        for k in range(PASSES // CHUNK):
-            h_tile = keep.tile([P, CHUNK, PACK, EDGES], BF16, name="h%d" % k)
-            nc.sync.dma_start(out=h_tile[:], in_=h_view[:, k * CHUNK : (k + 1) * CHUNK])
-            h_tiles.append(h_tile)
-            for cc in range(CHUNK):
-                c = k * CHUNK + cc
-                for t in range(PACK):
-                    row = h_tile[:, cc, t, :]
-                    if t < ROWS_ON_VECTOR:
-                        unread_v = work.tile([P, EDGES], BF16, tag="unread_v", bufs=4)
-                        nc.vector.tensor_scalar(
-                            out=unread_v[:], in0=row, scalar1=1.0, scalar2=None,
-                            op0=MULT, op1=ADD, accum_out=sum_v[:, c, t : t + 1],
-                        )
-                    else:
-                        unread_s = work.tile([P, EDGES], BF16, tag="unread_s", bufs=2)
-                        nc.scalar.activation(
-                            out=unread_s[:], in_=row, func=ACT.Copy,
-                            accum_out=sum_s[:, c, t - ROWS_ON_VECTOR : t - ROWS_ON_VECTOR + 1],
-                        )
-                    for j in range(TILES):
-                        nc.tensor.matmul(
-                            out=col_ps[j][:],
-                            lhsT=h_tile[:, cc, t, j * P : (j + 1) * P],
-                            rhs=ones[:],
-                            start=(c == 0 and t == 0),
-                            stop=(c == PASSES - 1 and t == PACK - 1),
-                        )
-                if (c + 1) % A_BATCH == 0:
-                    batch = slice(c + 1 - A_BATCH, c + 1)
-                    nc.vector.tensor_scalar_max(
-                        out=deg_v[:, batch, :ROWS_ON_VECTOR], in0=sum_v[:, batch, :], scalar1=1.0
+        for c in range(PASSES):
+            h_rows = keep.tile([P, PACK, EDGES], BF16, name="h%d" % c)
+            nc.sync.dma_start(out=h_rows[:], in_=h_view[:, c])
+            h_tiles.append(h_rows)
+            for t in range(PACK):
+                if t < ROWS_ON_VECTOR:
+                    unread_v = work.tile([P, EDGES], BF16, tag="unread_v", bufs=4)
+                    nc.vector.tensor_scalar(
+                        out=unread_v[:], in0=h_rows[:, t, :], scalar1=1.0, scalar2=None,
+                        op0=MULT, op1=ADD, accum_out=sum_v[:, c, t : t + 1],
                     )
-                    nc.vector.tensor_scalar_max(
-                        out=deg_v[:, batch, ROWS_ON_VECTOR:], in0=sum_s[:, batch, :], scalar1=1.0
+                else:
+                    unread_s = work.tile([P, EDGES], BF16, tag="unread_s", bufs=4)
+                    nc.scalar.activation(
+                        out=unread_s[:], in_=h_rows[:, t, :], func=ACT.Copy,
+                        accum_out=sum_s[:, c, t - ROWS_ON_VECTOR : t - ROWS_ON_VECTOR + 1],
                     )
-                    nc.scalar.activation(out=root_v[:, batch, :], in_=deg_v[:, batch, :], func=ACT.Sqrt)
-                    nc.vector.reciprocal(out=a[:, batch, :], in_=root_v[:, batch, :])
+                for j in range(TILES):
+                    nc.tensor.matmul(
+                        out=col_ps[j][:],
+                        lhsT=h_rows[:, t, j * P : (j + 1) * P],
+                        rhs=ones[:],
+                        start=(c == 0 and t == 0),
+                        stop=(c == PASSES - 1 and t == PACK - 1),
+                    )
+            if (c + 1) % A_BATCH == 0:
+                batch = slice(c + 1 - A_BATCH, c + 1)
+                nc.vector.tensor_scalar_max(
+                    out=deg_v[:, batch, :ROWS_ON_VECTOR], in0=sum_v[:, batch, :], scalar1=1.0
+                )
+                nc.vector.tensor_scalar_max(
+                    out=deg_v[:, batch, ROWS_ON_VECTOR:], in0=sum_s[:, batch, :], scalar1=1.0
+                )
+                nc.scalar.activation(out=root_v[:, batch, :], in_=deg_v[:, batch, :], func=ACT.Sqrt)
+                nc.vector.reciprocal(out=a[:, batch, :], in_=root_v[:, batch, :])
 
         deg_e = keep.tile([P, TILES], F32)
         root_e = keep.tile([P, TILES], F32)
@@ -132,14 +137,14 @@ def tile_hypergraphgpslayer_pb_k_kernel(
                 stop=True,
             )
 
-        w_rows = work.tile([P, PACK, DIM], BF16, tag="x_rows", bufs=4)
+        w_rows = rows_tile("w_rows", 1)
         nc.sync.dma_start(out=w_rows[:], in_=Wr.rearrange("(t p) n -> p t n", p=P))
-        w_grouped = work.tile([P, DIM, PACK], BF16, tag="x_grouped", align_bytes=64)
-        regroup(nc.scalar.copy, w_grouped, w_rows, slice(0, DIM))
+        w_grouped = grouped_tile("w_grouped")
+        nc.scalar.copy(out=by_column(w_grouped, all_cols), in_=by_row(w_rows, all_cols))
         w_codes, w_scales = packed_tiles(keep, "w")
         quantise(nc, w_codes, w_scales, w_grouped)
 
-        x1_rows = work.tile([P, TILES, DIM], BF16, tag="x_rows", bufs=4)
+        x1_rows = rows_tile("x1_rows", 1)
         nc.sync.dma_start(out=x1_rows[:], in_=x_1_new.rearrange("(i p) d -> p i d", p=P))
         br_all = keep.tile([P, DIM], BF16)
         nc.sync.dma_start(out=br_all[:], in_=br.partition_broadcast(P))
@@ -151,30 +156,41 @@ def tile_hypergraphgpslayer_pb_k_kernel(
             )
 
         ret_ps = [psum.tile([P, EDGES], F32, name="ret%d" % j, tag="acc%d" % j) for j in range(TILES)]
-        grouped_of = {}
+        x_rows_of = {}
+        x_grouped_of = {}
+        h_grouped_of = {}
 
-        def prepare(c):
-            x_rows = work.tile([P, PACK, DIM], BF16, tag="x_rows", bufs=4)
-            nc.sync.dma_start(out=x_rows[:], in_=x_view[:, c])
-            x_grouped = work.tile([P, DIM, PACK], BF16, tag="x_grouped", align_bytes=64)
-            regroup(nc.vector.tensor_copy, x_grouped, x_rows, slice(0, X_COLS_ON_VECTOR))
-            regroup(nc.scalar.copy, x_grouped, x_rows, slice(X_COLS_ON_VECTOR, DIM))
-            h_norm = work.tile([P, PACK, EDGES], BF16, tag="h_norm")
+        def fetch_x(c):
+            x_rows_of[c] = rows_tile("x_rows", X_AHEAD)
+            nc.sync.dma_start(out=x_rows_of[c][:], in_=x_view[:, c])
+
+        def regroup_x(c):
+            x_grouped_of[c] = grouped_tile("x_grouped")
+            on_gpsimd = slice(0, X_COLS_ON_GPSIMD)
+            on_scalar = slice(X_COLS_ON_GPSIMD, DIM)
+            nc.gpsimd.tensor_scalar(
+                out=by_column(x_grouped_of[c], on_gpsimd), in0=by_row(x_rows_of[c], on_gpsimd),
+                scalar1=1.0, scalar2=0.0, op0=MULT, op1=ADD,
+            )
+            nc.scalar.copy(out=by_column(x_grouped_of[c], on_scalar), in_=by_row(x_rows_of[c], on_scalar))
+            if c + X_AHEAD < PASSES:
+                fetch_x(c + X_AHEAD)
+
+        def normalise_h(c):
+            h_norm = rows_tile("h_norm", 2)
             for t in range(PACK):
                 nc.vector.scalar_tensor_tensor(
-                    out=h_norm[:, t, :], in0=h_tiles[c // CHUNK][:, c % CHUNK, t, :],
+                    out=h_norm[:, t, :], in0=h_tiles[c][:, t, :],
                     scalar=a[:, c, t : t + 1], in1=b_ps[:], op0=MULT, op1=MULT,
                 )
-            h_grouped = work.tile([P, EDGES, PACK], BF16, tag="h_grouped", align_bytes=64)
-            regroup(nc.scalar.copy, h_grouped, h_norm, slice(0, EDGES))
-            grouped_of[c] = (x_grouped, h_grouped)
+            h_grouped_of[c] = grouped_tile("h_grouped")
+            nc.scalar.copy(out=by_column(h_grouped_of[c], all_cols), in_=by_row(h_norm, all_cols))
 
         def multiply(c):
-            x_grouped, h_grouped = grouped_of[c]
-            x_codes, x_scales = packed_tiles(work, "x")
-            quantise(nc, x_codes, x_scales, x_grouped)
             h_codes, h_scales = packed_tiles(work, "h")
-            quantise(nc, h_codes, h_scales, h_grouped)
+            quantise(nc, h_codes, h_scales, h_grouped_of[c])
+            x_codes, x_scales = packed_tiles(work, "x")
+            quantise(nc, x_codes, x_scales, x_grouped_of[c])
             for j in range(TILES):
                 cols = slice(j * P, (j + 1) * P)
                 nc.tensor.matmul_mx(
@@ -184,35 +200,42 @@ def tile_hypergraphgpslayer_pb_k_kernel(
                     start=(c == 0), stop=(c == PASSES - 1),
                 )
 
-        prepare(0)
-        for c in range(1, PASSES):
-            prepare(c)
-            multiply(c - 1)
-        multiply(PASSES - 1)
+        with tc.manual_schedule():
+            for c in range(X_AHEAD):
+                fetch_x(c)
+            regroup_x(0)
+            normalise_h(0)
+            regroup_x(1)
+            for c in range(1, PASSES):
+                normalise_h(c)
+                multiply(c - 1)
+                if c + 1 < PASSES:
+                    regroup_x(c + 1)
+            multiply(PASSES - 1)
 
-        r_rows = work.tile([P, PACK, EDGES], BF16, tag="h_norm")
-        for j in range(TILES):
-            if j % 2 == 0:
-                nc.vector.tensor_copy(out=r_rows[:, j, :], in_=ret_ps[j][:])
-            else:
-                nc.scalar.copy(out=r_rows[:, j, :], in_=ret_ps[j][:])
-        r_grouped = work.tile([P, EDGES, PACK], BF16, tag="h_grouped", align_bytes=64)
-        regroup(nc.vector.tensor_copy, r_grouped, r_rows, slice(0, EDGES))
-        r_codes, r_scales = packed_tiles(work, "h")
-        quantise(nc, r_codes, r_scales, r_grouped)
+            r_rows = rows_tile("h_norm", 2)
+            for j in range(TILES):
+                if j % 2 == 0:
+                    nc.vector.tensor_copy(out=r_rows[:, j, :], in_=ret_ps[j][:])
+                else:
+                    nc.scalar.copy(out=r_rows[:, j, :], in_=ret_ps[j][:])
+            r_grouped = grouped_tile("h_grouped")
+            nc.vector.tensor_copy(out=by_column(r_grouped, all_cols), in_=by_row(r_rows, all_cols))
+            r_codes, r_scales = packed_tiles(work, "h")
+            quantise(nc, r_codes, r_scales, r_grouped)
 
-        for i in range(TILES):
-            cols = slice(i * P, (i + 1) * P)
-            upd_ps = psum.tile([P, DIM], F32, name="upd%d" % i, tag="acc%d" % i)
-            nc.tensor.matmul_mx(
-                out=upd_ps[:],
-                lhsT=r_codes[:, cols].bitcast(FP8X4), lhsT_scale=r_scales[:, cols],
-                rhs=w_codes[:].bitcast(FP8X4), rhs_scale=w_scales[:],
-                start=True, stop=True,
-            )
-            result = work.tile([P, DIM], F32, tag="x_rows", bufs=4)
-            nc.vector.scalar_tensor_tensor(
-                out=result[:], in0=upd_ps[:], scalar=gate[:, 0:1], in1=rest[:, i, :],
-                op0=MULT, op1=ADD,
-            )
-            nc.sync.dma_start(out=out[cols, :], in_=result[:])
+            for i in range(TILES):
+                cols = slice(i * P, (i + 1) * P)
+                upd_ps = psum.tile([P, DIM], F32, name="upd%d" % i, tag="acc%d" % i)
+                nc.tensor.matmul_mx(
+                    out=upd_ps[:],
+                    lhsT=r_codes[:, cols].bitcast(FP8X4), lhsT_scale=r_scales[:, cols],
+                    rhs=w_codes[:].bitcast(FP8X4), rhs_scale=w_scales[:],
+                    start=True, stop=True,
+                )
+                result = work.tile([P, DIM], F32, tag="result", bufs=4)
+                nc.vector.scalar_tensor_tensor(
+                    out=result[:], in0=upd_ps[:], scalar=gate[:, 0:1], in1=rest[:, i, :],
+                    op0=MULT, op1=ADD,
+                )
+                nc.sync.dma_start(out=out[cols, :], in_=result[:])

@@ -18,12 +18,13 @@ PACK = 4
 K_PASS = P * PACK
 PASSES = NODES // K_PASS
 TILES = 4
-ROWS_ON_VECTOR = 2
 A_BATCH = 8
 ONES_COLS = 32
 RUN = 4
 X_COLS_ON_GPSIMD = 320
+R_COLS_ON_VECTOR = 320
 X_AHEAD = 4
+MAX = mybir.AluOpType.max
 
 FLOPS = 2 * NODES * EDGES * DIM + 2 * EDGES * DIM * DIM
 
@@ -36,12 +37,8 @@ def by_row(rows, cols):
     return rows[:, :, cols].rearrange("p t (c i) -> p c t i", i=RUN)
 
 
-def quantise(nc, codes, scales, grouped):
-    nc.vector.quantize_mx(
-        out=codes[:].bitcast(FP8X4),
-        scales=scales[:],
-        in_=grouped[:].rearrange("p w t -> p (w t)"),
-    )
+def scalar_sums_row(c, t):
+    return t == 3 or (t == 2 and c % 2 == 1)
 
 
 def tile_hypergraphgpslayer_pb_k_kernel(
@@ -57,28 +54,45 @@ def tile_hypergraphgpslayer_pb_k_kernel(
         work = stack.enter_context(tc.tile_pool(name="work", bufs=2))
         psum = stack.enter_context(tc.psum_pool(name="psum", bufs=1))
 
-        def rows_tile(tag, bufs):
-            return work.tile([P, PACK, 512], BF16, name=tag, tag=tag, bufs=bufs)
-
-        def grouped_tile(tag):
-            return work.tile([P, 512, PACK], BF16, name=tag, tag=tag, align_bytes=64)
-
-        def packed_tiles(pool, tag):
-            codes = pool.tile([P, 512], U32, name=tag + "_codes", tag=tag + "_codes", align_bytes=64)
-            scales = pool.tile([P, 512], U8, name=tag + "_scales", tag=tag + "_scales", align_bytes=64)
-            return codes, scales
-
         gate_raw = keep.tile([P, 1], BF16)
         nc.sync.dma_start(out=gate_raw[:], in_=gate_return.partition_broadcast(P))
-        gate = keep.tile([P, 1], F32)
-        nc.scalar.activation(out=gate[:], in_=gate_raw[:], func=ACT.Tanh)
-        ones = keep.tile([P, ONES_COLS], BF16)
+        br_row = keep.tile([P, DIM], BF16)
+        nc.vector.memset(br_row[:], 0.0)
+        nc.sync.dma_start(out=br_row[0:1, :], in_=br.rearrange("(o d) -> o d", o=1))
+        x1_rows = keep.tile([P, TILES, DIM], BF16)
+        nc.sync.dma_start(out=x1_rows[:], in_=x_1_new.rearrange("(i p) d -> p i d", p=P))
+        w_rows = keep.tile([P, PACK, DIM], BF16)
+        nc.sync.dma_start(out=w_rows[:], in_=Wr.rearrange("(t p) n -> p t n", p=P))
+
+        ones = keep.tile([P, P], BF16)
         nc.vector.memset(ones[:], 1.0)
         ident = keep.tile([P, P], F32)
         make_identity(nc, ident[:])
+        gate = keep.tile([P, 1], F32)
+        nc.scalar.activation(out=gate[:], in_=gate_raw[:], func=ACT.Tanh)
 
-        sum_v = keep.tile([P, PASSES, ROWS_ON_VECTOR], F32)
-        sum_s = keep.tile([P, PASSES, PACK - ROWS_ON_VECTOR], F32)
+        br_ps = psum.tile([P, DIM], F32, tag="bias")
+        nc.tensor.matmul(out=br_ps[:], lhsT=ones[:], rhs=br_row[:], start=True, stop=True)
+        rest = keep.tile([P, TILES, DIM], F32)
+        for i in range(TILES):
+            nc.vector.scalar_tensor_tensor(
+                out=rest[:, i, :], in0=br_ps[:], scalar=gate[:, 0:1], in1=x1_rows[:, i, :],
+                op0=MULT, op1=ADD,
+            )
+
+        w_grouped = keep.tile([P, DIM, PACK], BF16, align_bytes=64)
+        nc.scalar.copy(out=by_column(w_grouped, all_cols), in_=by_row(w_rows, all_cols))
+        w_codes = keep.tile([P, DIM], U32, align_bytes=64)
+        w_scales = keep.tile([P, DIM], U8, align_bytes=64)
+        nc.vector.quantize_mx(
+            out=w_codes[:].bitcast(FP8X4), scales=w_scales[:],
+            in_=w_grouped[:].rearrange("p w t -> p (w t)"),
+        )
+
+        sum_v = keep.tile([P, PASSES, PACK], F32)
+        sum_s = keep.tile([P, PASSES, PACK], F32)
+        nc.vector.memset(sum_v[:], 0.0)
+        nc.vector.memset(sum_s[:], 0.0)
         deg_v = keep.tile([P, PASSES, PACK], F32)
         root_v = keep.tile([P, PASSES, PACK], F32)
         a = keep.tile([P, PASSES, PACK], F32)
@@ -89,33 +103,31 @@ def tile_hypergraphgpslayer_pb_k_kernel(
             nc.sync.dma_start(out=h_rows[:], in_=h_view[:, c])
             h_tiles.append(h_rows)
             for t in range(PACK):
-                if t < ROWS_ON_VECTOR:
+                if scalar_sums_row(c, t):
+                    unread_s = work.tile([P, EDGES], BF16, tag="unread_s", bufs=4)
+                    nc.scalar.activation(
+                        out=unread_s[:], in_=h_rows[:, t, :], func=ACT.Copy,
+                        accum_out=sum_s[:, c, t : t + 1],
+                    )
+                else:
                     unread_v = work.tile([P, EDGES], BF16, tag="unread_v", bufs=4)
                     nc.vector.tensor_scalar(
                         out=unread_v[:], in0=h_rows[:, t, :], scalar1=1.0, scalar2=None,
                         op0=MULT, op1=ADD, accum_out=sum_v[:, c, t : t + 1],
                     )
-                else:
-                    unread_s = work.tile([P, EDGES], BF16, tag="unread_s", bufs=4)
-                    nc.scalar.activation(
-                        out=unread_s[:], in_=h_rows[:, t, :], func=ACT.Copy,
-                        accum_out=sum_s[:, c, t - ROWS_ON_VECTOR : t - ROWS_ON_VECTOR + 1],
-                    )
                 for j in range(TILES):
                     nc.tensor.matmul(
                         out=col_ps[j][:],
                         lhsT=h_rows[:, t, j * P : (j + 1) * P],
-                        rhs=ones[:],
+                        rhs=ones[:, :ONES_COLS],
                         start=(c == 0 and t == 0),
                         stop=(c == PASSES - 1 and t == PACK - 1),
                     )
             if (c + 1) % A_BATCH == 0:
                 batch = slice(c + 1 - A_BATCH, c + 1)
-                nc.vector.tensor_scalar_max(
-                    out=deg_v[:, batch, :ROWS_ON_VECTOR], in0=sum_v[:, batch, :], scalar1=1.0
-                )
-                nc.vector.tensor_scalar_max(
-                    out=deg_v[:, batch, ROWS_ON_VECTOR:], in0=sum_s[:, batch, :], scalar1=1.0
+                nc.vector.scalar_tensor_tensor(
+                    out=deg_v[:, batch, :], in0=sum_v[:, batch, :], scalar=1.0, in1=sum_s[:, batch, :],
+                    op0=MAX, op1=MAX,
                 )
                 nc.scalar.activation(out=root_v[:, batch, :], in_=deg_v[:, batch, :], func=ACT.Sqrt)
                 nc.vector.reciprocal(out=a[:, batch, :], in_=root_v[:, batch, :])
@@ -137,66 +149,51 @@ def tile_hypergraphgpslayer_pb_k_kernel(
                 stop=True,
             )
 
-        w_rows = rows_tile("w_rows", 1)
-        nc.sync.dma_start(out=w_rows[:], in_=Wr.rearrange("(t p) n -> p t n", p=P))
-        w_grouped = grouped_tile("w_grouped")
-        nc.scalar.copy(out=by_column(w_grouped, all_cols), in_=by_row(w_rows, all_cols))
-        w_codes, w_scales = packed_tiles(keep, "w")
-        quantise(nc, w_codes, w_scales, w_grouped)
-
-        x1_rows = rows_tile("x1_rows", 1)
-        nc.sync.dma_start(out=x1_rows[:], in_=x_1_new.rearrange("(i p) d -> p i d", p=P))
-        br_all = keep.tile([P, DIM], BF16)
-        nc.sync.dma_start(out=br_all[:], in_=br.partition_broadcast(P))
-        rest = keep.tile([P, TILES, DIM], F32)
-        for i in range(TILES):
-            nc.vector.scalar_tensor_tensor(
-                out=rest[:, i, :], in0=br_all[:], scalar=gate[:, 0:1], in1=x1_rows[:, i, :],
-                op0=MULT, op1=ADD,
-            )
-
         ret_ps = [psum.tile([P, EDGES], F32, name="ret%d" % j, tag="acc%d" % j) for j in range(TILES)]
+        OF_H, OF_X = 0, 1
         x_rows_of = {}
-        x_grouped_of = {}
-        h_grouped_of = {}
+        grouped_of = {}
 
         def fetch_x(c):
-            x_rows_of[c] = rows_tile("x_rows", X_AHEAD)
+            x_rows_of[c] = work.tile([P, PACK, DIM], BF16, name="x_rows", tag="x_rows", bufs=X_AHEAD)
             nc.sync.dma_start(out=x_rows_of[c][:], in_=x_view[:, c])
 
         def regroup_x(c):
-            x_grouped_of[c] = grouped_tile("x_grouped")
+            grouped_of[c] = work.tile([P, 2, 512, PACK], BF16, name="grouped", tag="grouped", align_bytes=64)
+            x_grouped = grouped_of[c][:, OF_X]
             on_gpsimd = slice(0, X_COLS_ON_GPSIMD)
             on_scalar = slice(X_COLS_ON_GPSIMD, DIM)
             nc.gpsimd.tensor_scalar(
-                out=by_column(x_grouped_of[c], on_gpsimd), in0=by_row(x_rows_of[c], on_gpsimd),
+                out=by_column(x_grouped, on_gpsimd), in0=by_row(x_rows_of[c], on_gpsimd),
                 scalar1=1.0, scalar2=0.0, op0=MULT, op1=ADD,
             )
-            nc.scalar.copy(out=by_column(x_grouped_of[c], on_scalar), in_=by_row(x_rows_of[c], on_scalar))
+            nc.scalar.copy(out=by_column(x_grouped, on_scalar), in_=by_row(x_rows_of[c], on_scalar))
             if c + X_AHEAD < PASSES:
                 fetch_x(c + X_AHEAD)
 
         def normalise_h(c):
-            h_norm = rows_tile("h_norm", 2)
+            h_norm = work.tile([P, PACK, EDGES], BF16, tag="h_norm")
             for t in range(PACK):
                 nc.vector.scalar_tensor_tensor(
                     out=h_norm[:, t, :], in0=h_tiles[c][:, t, :],
                     scalar=a[:, c, t : t + 1], in1=b_ps[:], op0=MULT, op1=MULT,
                 )
-            h_grouped_of[c] = grouped_tile("h_grouped")
-            nc.scalar.copy(out=by_column(h_grouped_of[c], all_cols), in_=by_row(h_norm, all_cols))
+            nc.scalar.copy(out=by_column(grouped_of[c][:, OF_H], all_cols), in_=by_row(h_norm, all_cols))
 
         def multiply(c):
-            h_codes, h_scales = packed_tiles(work, "h")
-            quantise(nc, h_codes, h_scales, h_grouped_of[c])
-            x_codes, x_scales = packed_tiles(work, "x")
-            quantise(nc, x_codes, x_scales, x_grouped_of[c])
+            codes = work.tile([P, 2, 512], U32, tag="codes", align_bytes=64)
+            scales = work.tile([P, 2, 512], U8, tag="scales", align_bytes=64)
+            nc.vector.quantize_mx(
+                out=codes[:].rearrange("p o w -> p (o w)").bitcast(FP8X4),
+                scales=scales[:].rearrange("p o w -> p (o w)"),
+                in_=grouped_of[c][:].rearrange("p o w t -> p (o w t)"),
+            )
             for j in range(TILES):
                 cols = slice(j * P, (j + 1) * P)
                 nc.tensor.matmul_mx(
                     out=ret_ps[j][:],
-                    lhsT=x_codes[:, cols].bitcast(FP8X4), lhsT_scale=x_scales[:, cols],
-                    rhs=h_codes[:].bitcast(FP8X4), rhs_scale=h_scales[:],
+                    lhsT=codes[:, OF_X, cols].bitcast(FP8X4), lhsT_scale=scales[:, OF_X, cols],
+                    rhs=codes[:, OF_H, :].bitcast(FP8X4), rhs_scale=scales[:, OF_H, :],
                     start=(c == 0), stop=(c == PASSES - 1),
                 )
 
@@ -213,16 +210,23 @@ def tile_hypergraphgpslayer_pb_k_kernel(
                     regroup_x(c + 1)
             multiply(PASSES - 1)
 
-            r_rows = rows_tile("h_norm", 2)
+            r_rows = work.tile([P, PACK, EDGES], BF16, tag="h_norm")
             for j in range(TILES):
                 if j % 2 == 0:
                     nc.vector.tensor_copy(out=r_rows[:, j, :], in_=ret_ps[j][:])
                 else:
                     nc.scalar.copy(out=r_rows[:, j, :], in_=ret_ps[j][:])
-            r_grouped = grouped_tile("h_grouped")
-            nc.vector.tensor_copy(out=by_column(r_grouped, all_cols), in_=by_row(r_rows, all_cols))
-            r_codes, r_scales = packed_tiles(work, "h")
-            quantise(nc, r_codes, r_scales, r_grouped)
+            r_grouped = keep.tile([P, EDGES, PACK], BF16, align_bytes=64)
+            on_vector = slice(0, R_COLS_ON_VECTOR)
+            on_scalar = slice(R_COLS_ON_VECTOR, EDGES)
+            nc.vector.tensor_copy(out=by_column(r_grouped, on_vector), in_=by_row(r_rows, on_vector))
+            nc.scalar.copy(out=by_column(r_grouped, on_scalar), in_=by_row(r_rows, on_scalar))
+            r_codes = keep.tile([P, EDGES], U32, align_bytes=64)
+            r_scales = keep.tile([P, EDGES], U8, align_bytes=64)
+            nc.vector.quantize_mx(
+                out=r_codes[:].bitcast(FP8X4), scales=r_scales[:],
+                in_=r_grouped[:].rearrange("p w t -> p (w t)"),
+            )
 
             for i in range(TILES):
                 cols = slice(i * P, (i + 1) * P)

@@ -7,6 +7,7 @@ BF16 = mybir.dt.bfloat16
 F32 = mybir.dt.float32
 U32 = mybir.dt.uint32
 U8 = mybir.dt.uint8
+I32 = mybir.dt.int32
 FP8X4 = mybir.dt.float8_e4m3fn_x4
 MULT = mybir.AluOpType.mult
 ADD = mybir.AluOpType.add
@@ -19,12 +20,23 @@ K_PASS = P * PACK
 PASSES = NODES // K_PASS
 TILES = 4
 A_BATCH = 8
-ONES_COLS = 32
+ONES_COLS = 1
 RUN = 4
-X_COLS_ON_GPSIMD = 320
+X_COLS_BESIDE_DIRECT = 384
+X_COLS_BESIDE_OUTER = 208
 R_COLS_ON_VECTOR = 320
+ROWS_AHEAD = 6
 X_AHEAD = 4
 MAX = mybir.AluOpType.max
+X = mybir.AxisListType.X
+
+PARTS = 3
+TERMS = [(0, 0), (0, 1), (0, 2), (1, 0), (1, 1), (2, 0)]
+
+WORD_UNIT = 16256.0
+WORD_BIAS = -16384.0
+WORDS = EDGES // 2
+ODD = 65536.0
 
 FLOPS = 2 * NODES * EDGES * DIM + 2 * EDGES * DIM * DIM
 
@@ -37,8 +49,37 @@ def by_row(rows, cols):
     return rows[:, :, cols].rearrange("p t (c i) -> p c t i", i=RUN)
 
 
+def is_outer(c):
+    return c < 24 and c % 2 == 1
+
+
+def second_sweep_order():
+    direct = [c for c in range(PASSES) if not is_outer(c)]
+    outer = [c for c in range(PASSES) if is_outer(c)]
+    order = []
+    for g in range(PASSES // 8):
+        d = direct[5 * g : 5 * g + 5]
+        o = outer[3 * g : 3 * g + 3]
+        order += [d[0], d[1], o[0], d[2], o[1], d[3], d[4], o[2]]
+    return order
+
+
+def split_parts(nc, pool, tag, wide, value, terms_index):
+    rest = value
+    n = value.shape[1]
+    for part in range(PARTS):
+        columns = [k for k in range(len(TERMS)) if TERMS[k][terms_index] == part]
+        for k in columns:
+            nc.vector.tensor_copy(out=wide[:, :, PACK * k : PACK * k + PACK], in_=rest)
+        if part + 1 < PARTS:
+            k = columns[0]
+            left = pool.tile([P, n, PACK], F32, name="left", tag=tag)
+            nc.vector.tensor_sub(out=left[:], in0=rest, in1=wide[:, :, PACK * k : PACK * k + PACK])
+            rest = left[:]
+
+
 def scalar_sums_row(c, t):
-    return t == 3 or (t == 2 and c % 2 == 1)
+    return t >= 2
 
 
 def tile_hypergraphgpslayer_pb_k_kernel(
@@ -59,19 +100,32 @@ def tile_hypergraphgpslayer_pb_k_kernel(
         br_row = keep.tile([P, DIM], BF16)
         nc.vector.memset(br_row[:], 0.0)
         nc.sync.dma_start(out=br_row[0:1, :], in_=br.rearrange("(o d) -> o d", o=1))
-        x1_rows = keep.tile([P, TILES, DIM], BF16)
+        x1_rows = work.tile([P, TILES, DIM], BF16, tag="rows", bufs=ROWS_AHEAD)
         nc.sync.dma_start(out=x1_rows[:], in_=x_1_new.rearrange("(i p) d -> p i d", p=P))
-        w_rows = keep.tile([P, PACK, DIM], BF16)
+        w_rows = work.tile([P, PACK, DIM], BF16, tag="rows", bufs=ROWS_AHEAD)
         nc.sync.dma_start(out=w_rows[:], in_=Wr.rearrange("(t p) n -> p t n", p=P))
 
         ones = keep.tile([P, P], BF16)
         nc.vector.memset(ones[:], 1.0)
         ident = keep.tile([P, P], F32)
         make_identity(nc, ident[:])
+        ident_bf = keep.tile([P, P], BF16)
+        nc.vector.tensor_copy(out=ident_bf[:], in_=ident[:])
+        pick = keep.tile([P, PACK], F32)
+        nc.vector.tensor_reduce(
+            out=pick[:], in_=ident[:].rearrange("p (m t) -> p t m", t=PACK), axis=X, op=ADD
+        )
+        outer_passes = [c for c in range(PASSES) if is_outer(c)]
+        a_parts = keep.tile([P, len(outer_passes), P], BF16)
+        nc.gpsimd.memset(a_parts[:], 0.0)
+        b_parts = keep.tile([P, TILES, P], BF16)
+        nc.gpsimd.memset(b_parts[:], 0.0)
+        a_rows = keep.tile([P, len(outer_passes), P], BF16)
+        b_rows = keep.tile([P, EDGES, PACK], BF16)
         gate = keep.tile([P, 1], F32)
         nc.scalar.activation(out=gate[:], in_=gate_raw[:], func=ACT.Tanh)
 
-        br_ps = psum.tile([P, DIM], F32, tag="bias")
+        br_ps = psum.tile([P, DIM], F32, tag="table", bufs=3)
         nc.tensor.matmul(out=br_ps[:], lhsT=ones[:], rhs=br_row[:], start=True, stop=True)
         rest = keep.tile([P, TILES, DIM], F32)
         for i in range(TILES):
@@ -80,7 +134,7 @@ def tile_hypergraphgpslayer_pb_k_kernel(
                 op0=MULT, op1=ADD,
             )
 
-        w_grouped = keep.tile([P, DIM, PACK], BF16, align_bytes=64)
+        w_grouped = work.tile([P, DIM, PACK], BF16, tag="grouped", align_bytes=64)
         nc.scalar.copy(out=by_column(w_grouped, all_cols), in_=by_row(w_rows, all_cols))
         w_codes = keep.tile([P, DIM], U32, align_bytes=64)
         w_scales = keep.tile([P, DIM], U8, align_bytes=64)
@@ -89,28 +143,39 @@ def tile_hypergraphgpslayer_pb_k_kernel(
             in_=w_grouped[:].rearrange("p w t -> p (w t)"),
         )
 
-        sum_v = keep.tile([P, PASSES, PACK], F32)
-        sum_s = keep.tile([P, PASSES, PACK], F32)
-        nc.vector.memset(sum_v[:], 0.0)
-        nc.vector.memset(sum_s[:], 0.0)
+        sum_v = keep.tile([P, PASSES, 2], F32)
+        sum_s = keep.tile([P, PASSES, 2], F32)
+        odd = keep.tile([P, PASSES, 2], I32)
+        both = keep.tile([P, PASSES, 2], I32)
         deg_v = keep.tile([P, PASSES, PACK], F32)
         root_v = keep.tile([P, PASSES, PACK], F32)
         a = keep.tile([P, PASSES, PACK], F32)
         col_ps = [psum.tile([P, ONES_COLS], F32, name="col%d" % j, tag="acc%d" % j) for j in range(TILES)]
         h_tiles = []
         for c in range(PASSES):
-            h_rows = keep.tile([P, PACK, EDGES], BF16, name="h%d" % c)
+            if is_outer(c):
+                h_rows = work.tile([P, PACK, EDGES], BF16, name="h_rows", tag="rows", bufs=ROWS_AHEAD)
+            else:
+                h_rows = keep.tile([P, PACK, EDGES], BF16, name="h%d" % c)
             nc.sync.dma_start(out=h_rows[:], in_=h_view[:, c])
-            h_tiles.append(h_rows)
+            if is_outer(c):
+                h_grouped = keep.tile([P, EDGES, PACK], BF16, name="h%d" % c)
+                nc.gpsimd.tensor_scalar(
+                    out=by_column(h_grouped, all_cols), in0=by_row(h_rows, all_cols),
+                    scalar1=1.0, scalar2=0.0, op0=MULT, op1=ADD,
+                )
+                h_tiles.append(h_grouped)
+            else:
+                h_tiles.append(h_rows)
             for t in range(PACK):
                 if scalar_sums_row(c, t):
-                    unread_s = work.tile([P, EDGES], BF16, tag="unread_s", bufs=4)
+                    unread_s = work.tile([P, WORDS], BF16, tag="unread_s")
                     nc.scalar.activation(
-                        out=unread_s[:], in_=h_rows[:, t, :], func=ACT.Copy,
-                        accum_out=sum_s[:, c, t : t + 1],
+                        out=unread_s[:], in_=h_rows[:, t, :].bitcast(U32), func=ACT.Copy,
+                        scale=1.0 / WORD_UNIT, bias=WORD_BIAS, accum_out=sum_s[:, c, t - 2 : t - 1],
                     )
                 else:
-                    unread_v = work.tile([P, EDGES], BF16, tag="unread_v", bufs=4)
+                    unread_v = work.tile([P, EDGES], BF16, tag="unread_v")
                     nc.vector.tensor_scalar(
                         out=unread_v[:], in0=h_rows[:, t, :], scalar1=1.0, scalar2=None,
                         op0=MULT, op1=ADD, accum_out=sum_v[:, c, t : t + 1],
@@ -125,12 +190,30 @@ def tile_hypergraphgpslayer_pb_k_kernel(
                     )
             if (c + 1) % A_BATCH == 0:
                 batch = slice(c + 1 - A_BATCH, c + 1)
+                nc.vector.tensor_scalar_max(out=deg_v[:, batch, 0:2], in0=sum_v[:, batch, :], scalar1=1.0)
+                nc.vector.tensor_scalar(
+                    out=odd[:, batch, :], in0=sum_s[:, batch, :],
+                    scalar1=-WORDS * WORD_BIAS, scalar2=1.0 / ODD, op0=ADD, op1=MULT,
+                )
                 nc.vector.scalar_tensor_tensor(
-                    out=deg_v[:, batch, :], in0=sum_v[:, batch, :], scalar=1.0, in1=sum_s[:, batch, :],
-                    op0=MAX, op1=MAX,
+                    out=both[:, batch, :], in0=odd[:, batch, :], scalar=1.0 - ODD, in1=sum_s[:, batch, :],
+                    op0=MULT, op1=ADD,
+                )
+                nc.vector.tensor_scalar(
+                    out=deg_v[:, batch, 2:4], in0=both[:, batch, :],
+                    scalar1=-WORDS * WORD_BIAS, scalar2=1.0, op0=ADD, op1=MAX,
                 )
                 nc.scalar.activation(out=root_v[:, batch, :], in_=deg_v[:, batch, :], func=ACT.Sqrt)
                 nc.vector.reciprocal(out=a[:, batch, :], in_=root_v[:, batch, :])
+                ready = [i for i in range(len(outer_passes)) if c + 1 - A_BATCH <= outer_passes[i] <= c]
+                if ready:
+                    some = slice(ready[0], ready[-1] + 1)
+                    a_outer = a[:, batch, :].rearrange("p (n two) t -> p n two t", two=2)[:, :, 1, :]
+                    split_parts(nc, work, "left_a", a_parts[:, some, :], a_outer, 0)
+                    a_ps = psum.tile([P, len(ready), P], BF16, name="a_ps", tag="table", bufs=3)
+                    for i in ready:
+                        nc.tensor.transpose(a_ps[:, i - ready[0], :], a_parts[:, i, :], ident_bf[:])
+                    nc.scalar.copy(out=a_rows[:, some, :], in_=a_ps[:])
 
         deg_e = keep.tile([P, TILES], F32)
         root_e = keep.tile([P, TILES], F32)
@@ -153,25 +236,66 @@ def tile_hypergraphgpslayer_pb_k_kernel(
         OF_H, OF_X = 0, 1
         x_rows_of = {}
         grouped_of = {}
+        tables_of = {}
+        order = second_sweep_order()
+        x_queue = list(order)
+        table_queue = [c for c in order if is_outer(c)]
 
         def fetch_x(c):
             x_rows_of[c] = work.tile([P, PACK, DIM], BF16, name="x_rows", tag="x_rows", bufs=X_AHEAD)
             nc.sync.dma_start(out=x_rows_of[c][:], in_=x_view[:, c])
 
+        def spread_b():
+            b_wide = b_col[:].unsqueeze(2).to_broadcast([P, TILES, PACK])
+            split_parts(nc, work, "left_b", b_parts[:], b_wide, 1)
+            parts_ps = psum.tile([P, EDGES], F32, name="parts_ps", tag="table", bufs=3)
+            for j in range(TILES):
+                nc.tensor.matmul(
+                    out=parts_ps[:, j * P : (j + 1) * P], lhsT=b_parts[:, j, :], rhs=ident_bf[:],
+                    start=True, stop=True,
+                )
+            nc.vector.tensor_tensor(
+                out=b_rows[:], in0=parts_ps[:].unsqueeze(2).to_broadcast([P, EDGES, PACK]),
+                in1=pick[:].unsqueeze(1).to_broadcast([P, EDGES, PACK]), op=MULT,
+            )
+
+        def make_table(c):
+            i = outer_passes.index(c)
+            tables_of[c] = []
+            for half in range(2):
+                table = psum.tile([P, 2, P, PACK], BF16, name="table", tag="table", bufs=3)
+                for q in range(2):
+                    edges = slice((2 * half + q) * P, (2 * half + q + 1) * P)
+                    nc.tensor.matmul(
+                        out=table[:, q].rearrange("p e t -> p (e t)"), lhsT=a_rows[:, i, :],
+                        rhs=b_rows[:, edges, :].rearrange("p e t -> p (e t)"), start=True, stop=True,
+                    )
+                tables_of[c].append(table)
+
         def regroup_x(c):
             grouped_of[c] = work.tile([P, 2, 512, PACK], BF16, name="grouped", tag="grouped", align_bytes=64)
             x_grouped = grouped_of[c][:, OF_X]
-            on_gpsimd = slice(0, X_COLS_ON_GPSIMD)
-            on_scalar = slice(X_COLS_ON_GPSIMD, DIM)
+            cut = X_COLS_BESIDE_OUTER if is_outer(c) else X_COLS_BESIDE_DIRECT
+            on_gpsimd = slice(0, cut)
+            on_scalar = slice(cut, DIM)
             nc.gpsimd.tensor_scalar(
                 out=by_column(x_grouped, on_gpsimd), in0=by_row(x_rows_of[c], on_gpsimd),
                 scalar1=1.0, scalar2=0.0, op0=MULT, op1=ADD,
             )
             nc.scalar.copy(out=by_column(x_grouped, on_scalar), in_=by_row(x_rows_of[c], on_scalar))
-            if c + X_AHEAD < PASSES:
-                fetch_x(c + X_AHEAD)
+            if x_queue:
+                fetch_x(x_queue.pop(0))
 
         def normalise_h(c):
+            if is_outer(c):
+                for half in range(2):
+                    edges = slice(half * 2 * P, (half + 1) * 2 * P)
+                    nc.vector.tensor_tensor(
+                        out=grouped_of[c][:, OF_H, edges, :].rearrange("p e t -> p (e t)"),
+                        in0=h_tiles[c][:, edges, :].rearrange("p e t -> p (e t)"),
+                        in1=tables_of[c][half][:].rearrange("p q e t -> p (q e t)"), op=MULT,
+                    )
+                return
             h_norm = work.tile([P, PACK, EDGES], BF16, tag="h_norm")
             for t in range(PACK):
                 nc.vector.scalar_tensor_tensor(
@@ -180,7 +304,7 @@ def tile_hypergraphgpslayer_pb_k_kernel(
                 )
             nc.scalar.copy(out=by_column(grouped_of[c][:, OF_H], all_cols), in_=by_row(h_norm, all_cols))
 
-        def multiply(c):
+        def multiply(c, first, last):
             codes = work.tile([P, 2, 512], U32, tag="codes", align_bytes=64)
             scales = work.tile([P, 2, 512], U8, tag="scales", align_bytes=64)
             nc.vector.quantize_mx(
@@ -194,21 +318,26 @@ def tile_hypergraphgpslayer_pb_k_kernel(
                     out=ret_ps[j][:],
                     lhsT=codes[:, OF_X, cols].bitcast(FP8X4), lhsT_scale=scales[:, OF_X, cols],
                     rhs=codes[:, OF_H, :].bitcast(FP8X4), rhs_scale=scales[:, OF_H, :],
-                    start=(c == 0), stop=(c == PASSES - 1),
+                    start=first, stop=last,
                 )
 
         with tc.manual_schedule():
-            for c in range(X_AHEAD):
-                fetch_x(c)
-            regroup_x(0)
-            normalise_h(0)
-            regroup_x(1)
-            for c in range(1, PASSES):
+            for n in range(X_AHEAD):
+                fetch_x(x_queue.pop(0))
+            regroup_x(order[0])
+            normalise_h(order[0])
+            regroup_x(order[1])
+            for n in range(1, PASSES):
+                c = order[n]
                 normalise_h(c)
-                multiply(c - 1)
-                if c + 1 < PASSES:
-                    regroup_x(c + 1)
-            multiply(PASSES - 1)
+                if n == 1:
+                    spread_b()
+                if (n == 1 or is_outer(c)) and table_queue:
+                    make_table(table_queue.pop(0))
+                multiply(order[n - 1], first=(n == 1), last=False)
+                if n + 1 < PASSES:
+                    regroup_x(order[n + 1])
+            multiply(order[-1], first=False, last=True)
 
             r_rows = work.tile([P, PACK, EDGES], BF16, tag="h_norm")
             for j in range(TILES):
@@ -216,18 +345,19 @@ def tile_hypergraphgpslayer_pb_k_kernel(
                     nc.vector.tensor_copy(out=r_rows[:, j, :], in_=ret_ps[j][:])
                 else:
                     nc.scalar.copy(out=r_rows[:, j, :], in_=ret_ps[j][:])
-            r_grouped = keep.tile([P, EDGES, PACK], BF16, align_bytes=64)
+            r_grouped = work.tile([P, EDGES, PACK], BF16, tag="grouped", align_bytes=64)
             on_vector = slice(0, R_COLS_ON_VECTOR)
             on_scalar = slice(R_COLS_ON_VECTOR, EDGES)
             nc.vector.tensor_copy(out=by_column(r_grouped, on_vector), in_=by_row(r_rows, on_vector))
             nc.scalar.copy(out=by_column(r_grouped, on_scalar), in_=by_row(r_rows, on_scalar))
-            r_codes = keep.tile([P, EDGES], U32, align_bytes=64)
-            r_scales = keep.tile([P, EDGES], U8, align_bytes=64)
+            r_codes = work.tile([P, EDGES], U32, tag="codes", align_bytes=64)
+            r_scales = work.tile([P, EDGES], U8, tag="scales", align_bytes=64)
             nc.vector.quantize_mx(
                 out=r_codes[:].bitcast(FP8X4), scales=r_scales[:],
                 in_=r_grouped[:].rearrange("p w t -> p (w t)"),
             )
 
+            result = work.tile([P, TILES, DIM], F32, tag="grouped", align_bytes=64)
             for i in range(TILES):
                 cols = slice(i * P, (i + 1) * P)
                 upd_ps = psum.tile([P, DIM], F32, name="upd%d" % i, tag="acc%d" % i)
@@ -237,9 +367,8 @@ def tile_hypergraphgpslayer_pb_k_kernel(
                     rhs=w_codes[:].bitcast(FP8X4), rhs_scale=w_scales[:],
                     start=True, stop=True,
                 )
-                result = work.tile([P, DIM], F32, tag="result", bufs=4)
                 nc.vector.scalar_tensor_tensor(
-                    out=result[:], in0=upd_ps[:], scalar=gate[:, 0:1], in1=rest[:, i, :],
+                    out=result[:, i, :], in0=upd_ps[:], scalar=gate[:, 0:1], in1=rest[:, i, :],
                     op0=MULT, op1=ADD,
                 )
-                nc.sync.dma_start(out=out[cols, :], in_=result[:])
+                nc.sync.dma_start(out=out[cols, :], in_=result[:, i, :])

@@ -49,6 +49,14 @@ def by_row(rows, cols):
     return rows[:, :, cols].rearrange("p t (c i) -> p c t i", i=RUN)
 
 
+def plain_column(grouped, cols):
+    return grouped[:, cols, :]
+
+
+def plain_row(rows, cols):
+    return rows[:, :, cols].rearrange("p t c -> p c t")
+
+
 def is_outer(c):
     return c < 24 and c % 2 == 1
 
@@ -161,7 +169,7 @@ def tile_hypergraphgpslayer_pb_k_kernel(
             if is_outer(c):
                 h_grouped = keep.tile([P, EDGES, PACK], BF16, name="h%d" % c)
                 nc.gpsimd.tensor_scalar(
-                    out=by_column(h_grouped, all_cols), in0=by_row(h_rows, all_cols),
+                    out=plain_column(h_grouped, all_cols), in0=plain_row(h_rows, all_cols),
                     scalar1=1.0, scalar2=0.0, op0=MULT, op1=ADD,
                 )
                 h_tiles.append(h_grouped)
@@ -279,7 +287,7 @@ def tile_hypergraphgpslayer_pb_k_kernel(
             on_gpsimd = slice(0, cut)
             on_scalar = slice(cut, DIM)
             nc.gpsimd.tensor_scalar(
-                out=by_column(x_grouped, on_gpsimd), in0=by_row(x_rows_of[c], on_gpsimd),
+                out=plain_column(x_grouped, on_gpsimd), in0=plain_row(x_rows_of[c], on_gpsimd),
                 scalar1=1.0, scalar2=0.0, op0=MULT, op1=ADD,
             )
             nc.scalar.copy(out=by_column(x_grouped, on_scalar), in_=by_row(x_rows_of[c], on_scalar))

@@ -168,10 +168,10 @@ def tile_hypergraphgpslayer_pb_k_kernel(
             nc.sync.dma_start(out=h_rows[:], in_=h_view[:, c])
             if is_outer(c):
                 h_grouped = keep.tile([P, EDGES, PACK], BF16, name="h%d" % c)
-                nc.gpsimd.tensor_scalar(
-                    out=plain_column(h_grouped, all_cols), in0=plain_row(h_rows, all_cols),
-                    scalar1=1.0, scalar2=0.0, op0=MULT, op1=ADD,
-                )
+                on_vector = slice(0, R_COLS_ON_VECTOR)
+                on_scalar = slice(R_COLS_ON_VECTOR, EDGES)
+                nc.vector.tensor_copy(out=by_column(h_grouped, on_vector), in_=by_row(h_rows, on_vector))
+                nc.scalar.copy(out=by_column(h_grouped, on_scalar), in_=by_row(h_rows, on_scalar))
                 h_tiles.append(h_grouped)
             else:
                 h_tiles.append(h_rows)

@@ -11,6 +11,8 @@ I32 = mybir.dt.int32
 FP8X4 = mybir.dt.float8_e4m3fn_x4
 MULT = mybir.AluOpType.mult
 ADD = mybir.AluOpType.add
+MAX = mybir.AluOpType.max
+X = mybir.AxisListType.X
 ACT = mybir.ActivationFunctionType
 
 NODES, EDGES, DIM = 16384, 512, 512
@@ -19,16 +21,17 @@ PACK = 4
 K_PASS = P * PACK
 PASSES = NODES // K_PASS
 TILES = 4
-A_BATCH = 8
-ONES_COLS = 1
+BATCH = 8
+EARLY = 24
+SUMMED_EARLY = 28
+LATE_BATCH = 4
 RUN = 4
-X_COLS_BESIDE_DIRECT = 384
-X_COLS_BESIDE_OUTER = 208
-R_COLS_ON_VECTOR = 320
+X_COLS_BESIDE_DIRECT = 320
+X_COLS_BESIDE_OUTER = 160
+R_COLS_ON_VECTOR = 160
 ROWS_AHEAD = 6
+W_AT = 15
 X_AHEAD = 4
-MAX = mybir.AluOpType.max
-X = mybir.AxisListType.X
 
 PARTS = 3
 TERMS = [(0, 0), (0, 1), (0, 2), (1, 0), (1, 1), (2, 0)]
@@ -37,6 +40,7 @@ WORD_UNIT = 16256.0
 WORD_BIAS = -16384.0
 WORDS = EDGES // 2
 ODD = 65536.0
+V_ROWS = 1
 
 FLOPS = 2 * NODES * EDGES * DIM + 2 * EDGES * DIM * DIM
 
@@ -49,16 +53,8 @@ def by_row(rows, cols):
     return rows[:, :, cols].rearrange("p t (c i) -> p c t i", i=RUN)
 
 
-def plain_column(grouped, cols):
-    return grouped[:, cols, :]
-
-
-def plain_row(rows, cols):
-    return rows[:, :, cols].rearrange("p t c -> p c t")
-
-
 def is_outer(c):
-    return c < 24 and c % 2 == 1
+    return c < EARLY and c % 2 == 1
 
 
 def second_sweep_order():
@@ -68,7 +64,7 @@ def second_sweep_order():
     for g in range(PASSES // 8):
         d = direct[5 * g : 5 * g + 5]
         o = outer[3 * g : 3 * g + 3]
-        order += [d[0], d[1], o[0], d[2], o[1], d[3], d[4], o[2]]
+        order += [d[0], d[1], d[2], o[0], d[3], o[1], d[4], o[2]]
     return order
 
 
@@ -86,10 +82,6 @@ def split_parts(nc, pool, tag, wide, value, terms_index):
             rest = left[:]
 
 
-def scalar_sums_row(c, t):
-    return t >= 2
-
-
 def tile_hypergraphgpslayer_pb_k_kernel(
     tc, x_0_local, x_1_new, incidence_1, Wr, br, gate_return, out
 ):
@@ -97,147 +89,169 @@ def tile_hypergraphgpslayer_pb_k_kernel(
     h_view = incidence_1.rearrange("(c p t) e -> p c t e", p=P, t=PACK)
     x_view = x_0_local.rearrange("(c p t) d -> p c t d", p=P, t=PACK)
     all_cols = slice(0, 512)
+    order = second_sweep_order()
+    outer_passes = [c for c in range(PASSES) if is_outer(c)]
 
     with ExitStack() as stack:
         keep = stack.enter_context(tc.tile_pool(name="keep", bufs=1))
         work = stack.enter_context(tc.tile_pool(name="work", bufs=2))
         psum = stack.enter_context(tc.psum_pool(name="psum", bufs=1))
+        stack.enter_context(tc.manual_schedule())
 
         gate_raw = keep.tile([P, 1], BF16)
         nc.sync.dma_start(out=gate_raw[:], in_=gate_return.partition_broadcast(P))
         br_row = keep.tile([P, DIM], BF16)
         nc.vector.memset(br_row[:], 0.0)
         nc.sync.dma_start(out=br_row[0:1, :], in_=br.rearrange("(o d) -> o d", o=1))
-        x1_rows = work.tile([P, TILES, DIM], BF16, tag="rows", bufs=ROWS_AHEAD)
-        nc.sync.dma_start(out=x1_rows[:], in_=x_1_new.rearrange("(i p) d -> p i d", p=P))
-        w_rows = work.tile([P, PACK, DIM], BF16, tag="rows", bufs=ROWS_AHEAD)
-        nc.sync.dma_start(out=w_rows[:], in_=Wr.rearrange("(t p) n -> p t n", p=P))
 
         ones = keep.tile([P, P], BF16)
         nc.vector.memset(ones[:], 1.0)
         ident = keep.tile([P, P], F32)
         make_identity(nc, ident[:])
-        ident_bf = keep.tile([P, P], BF16)
-        nc.vector.tensor_copy(out=ident_bf[:], in_=ident[:])
-        pick = keep.tile([P, PACK], F32)
-        nc.vector.tensor_reduce(
-            out=pick[:], in_=ident[:].rearrange("p (m t) -> p t m", t=PACK), axis=X, op=ADD
-        )
-        outer_passes = [c for c in range(PASSES) if is_outer(c)]
         a_parts = keep.tile([P, len(outer_passes), P], BF16)
         nc.gpsimd.memset(a_parts[:], 0.0)
         b_parts = keep.tile([P, TILES, P], BF16)
         nc.gpsimd.memset(b_parts[:], 0.0)
         a_rows = keep.tile([P, len(outer_passes), P], BF16)
         b_rows = keep.tile([P, EDGES, PACK], BF16)
+        ident_bf = keep.tile([P, P], BF16)
+        nc.vector.tensor_copy(out=ident_bf[:], in_=ident[:])
+        pick = keep.tile([P, PACK], F32)
+        nc.vector.tensor_reduce(
+            out=pick[:], in_=ident[:].rearrange("p (m t) -> p t m", t=PACK), axis=X, op=ADD
+        )
         gate = keep.tile([P, 1], F32)
         nc.scalar.activation(out=gate[:], in_=gate_raw[:], func=ACT.Tanh)
 
         br_ps = psum.tile([P, DIM], F32, tag="table", bufs=3)
         nc.tensor.matmul(out=br_ps[:], lhsT=ones[:], rhs=br_row[:], start=True, stop=True)
         rest = keep.tile([P, TILES, DIM], F32)
-        for i in range(TILES):
-            nc.vector.scalar_tensor_tensor(
-                out=rest[:, i, :], in0=br_ps[:], scalar=gate[:, 0:1], in1=x1_rows[:, i, :],
-                op0=MULT, op1=ADD,
-            )
-
-        w_grouped = work.tile([P, DIM, PACK], BF16, tag="grouped", align_bytes=64)
-        nc.scalar.copy(out=by_column(w_grouped, all_cols), in_=by_row(w_rows, all_cols))
         w_codes = keep.tile([P, DIM], U32, align_bytes=64)
         w_scales = keep.tile([P, DIM], U8, align_bytes=64)
-        nc.vector.quantize_mx(
-            out=w_codes[:].bitcast(FP8X4), scales=w_scales[:],
-            in_=w_grouped[:].rearrange("p w t -> p (w t)"),
-        )
 
-        sum_v = keep.tile([P, PASSES, 2], F32)
-        sum_s = keep.tile([P, PASSES, 2], F32)
-        odd = keep.tile([P, PASSES, 2], I32)
-        both = keep.tile([P, PASSES, 2], I32)
+        sum_v = keep.tile([P, EARLY, V_ROWS], F32)
+        sum_s = keep.tile([P, PASSES, PACK], F32)
+        odd = keep.tile([P, PASSES, PACK], I32)
+        both = keep.tile([P, PASSES, PACK], I32)
         deg_v = keep.tile([P, PASSES, PACK], F32)
         root_v = keep.tile([P, PASSES, PACK], F32)
         a = keep.tile([P, PASSES, PACK], F32)
-        col_ps = [psum.tile([P, ONES_COLS], F32, name="col%d" % j, tag="acc%d" % j) for j in range(TILES)]
+        col_ps = [psum.tile([P, 1], F32, name="col%d" % j, tag="acc%d" % j) for j in range(TILES)]
         h_tiles = []
+        turned = {}
+
+        def sum_by_words(h_rows, c, t):
+            unread = work.tile([P, WORDS], BF16, name="unread", tag="unread_s")
+            nc.scalar.activation(
+                out=unread[:], in_=h_rows[:, t, :].bitcast(U32), func=ACT.Copy,
+                scale=1.0 / WORD_UNIT, bias=WORD_BIAS, accum_out=sum_s[:, c, t : t + 1],
+            )
+
+        def degrees(batch, first_word_row):
+            if first_word_row:
+                nc.vector.tensor_scalar_max(
+                    out=deg_v[:, batch, 0:first_word_row], in0=sum_v[:, batch, :], scalar1=1.0
+                )
+            rows = slice(first_word_row, PACK)
+            nc.vector.tensor_scalar(
+                out=odd[:, batch, rows], in0=sum_s[:, batch, rows],
+                scalar1=-WORDS * WORD_BIAS, scalar2=1.0 / ODD, op0=ADD, op1=MULT,
+            )
+            nc.vector.scalar_tensor_tensor(
+                out=both[:, batch, rows], in0=odd[:, batch, rows], scalar=1.0 - ODD,
+                in1=sum_s[:, batch, rows], op0=MULT, op1=ADD,
+            )
+            nc.vector.tensor_scalar(
+                out=deg_v[:, batch, rows], in0=both[:, batch, rows],
+                scalar1=-WORDS * WORD_BIAS, scalar2=1.0, op0=ADD, op1=MAX,
+            )
+
+        def roots(batch):
+            nc.scalar.activation(out=root_v[:, batch, :], in_=deg_v[:, batch, :], func=ACT.Sqrt)
+
+        def inverses(batch):
+            nc.vector.reciprocal(out=a[:, batch, :], in_=root_v[:, batch, :])
+
+        def split_a(batch):
+            some = slice(batch.start // 2, batch.stop // 2)
+            a_outer = a[:, batch, :].rearrange("p (n two) t -> p n two t", two=2)[:, :, 1, :]
+            split_parts(nc, work, "left_a", a_parts[:, some, :], a_outer, 0)
+
+        def turn_a(batch):
+            a_ps = psum.tile([P, BATCH // 2, P], BF16, name="a_ps", tag="table", bufs=3)
+            for i in range(BATCH // 2):
+                nc.tensor.transpose(a_ps[:, i, :], a_parts[:, batch.start // 2 + i, :], ident_bf[:])
+            turned[batch.start] = a_ps
+
+        def keep_a(batch):
+            some = slice(batch.start // 2, batch.stop // 2)
+            nc.scalar.copy(out=a_rows[:, some, :], in_=turned[batch.start][:])
+
         for c in range(PASSES):
             if is_outer(c):
                 h_rows = work.tile([P, PACK, EDGES], BF16, name="h_rows", tag="rows", bufs=ROWS_AHEAD)
             else:
                 h_rows = keep.tile([P, PACK, EDGES], BF16, name="h%d" % c)
             nc.sync.dma_start(out=h_rows[:], in_=h_view[:, c])
-            if is_outer(c):
-                h_grouped = keep.tile([P, EDGES, PACK], BF16, name="h%d" % c)
-                on_vector = slice(0, R_COLS_ON_VECTOR)
-                on_scalar = slice(R_COLS_ON_VECTOR, EDGES)
-                nc.vector.tensor_copy(out=by_column(h_grouped, on_vector), in_=by_row(h_rows, on_vector))
-                nc.scalar.copy(out=by_column(h_grouped, on_scalar), in_=by_row(h_rows, on_scalar))
-                h_tiles.append(h_grouped)
-            else:
-                h_tiles.append(h_rows)
+            if c == 3:
+                x1_rows = work.tile([P, TILES, DIM], BF16, tag="rows", bufs=ROWS_AHEAD)
+                nc.sync.dma_start(out=x1_rows[:], in_=x_1_new.rearrange("(i p) d -> p i d", p=P))
             for t in range(PACK):
-                if scalar_sums_row(c, t):
-                    unread_s = work.tile([P, WORDS], BF16, tag="unread_s")
-                    nc.scalar.activation(
-                        out=unread_s[:], in_=h_rows[:, t, :].bitcast(U32), func=ACT.Copy,
-                        scale=1.0 / WORD_UNIT, bias=WORD_BIAS, accum_out=sum_s[:, c, t - 2 : t - 1],
+                for j in range(TILES):
+                    nc.tensor.matmul(
+                        out=col_ps[j][:],
+                        lhsT=h_rows[:, t, j * P : (j + 1) * P],
+                        rhs=ones[:, :1],
+                        start=(c == 0 and t == 0),
+                        stop=(c == PASSES - 1 and t == PACK - 1),
                     )
-                else:
+            if c < EARLY:
+                for t in range(V_ROWS):
                     unread_v = work.tile([P, EDGES], BF16, tag="unread_v")
                     nc.vector.tensor_scalar(
                         out=unread_v[:], in0=h_rows[:, t, :], scalar1=1.0, scalar2=None,
                         op0=MULT, op1=ADD, accum_out=sum_v[:, c, t : t + 1],
                     )
-                for j in range(TILES):
-                    nc.tensor.matmul(
-                        out=col_ps[j][:],
-                        lhsT=h_rows[:, t, j * P : (j + 1) * P],
-                        rhs=ones[:, :ONES_COLS],
-                        start=(c == 0 and t == 0),
-                        stop=(c == PASSES - 1 and t == PACK - 1),
-                    )
-            if (c + 1) % A_BATCH == 0:
-                batch = slice(c + 1 - A_BATCH, c + 1)
-                nc.vector.tensor_scalar_max(out=deg_v[:, batch, 0:2], in0=sum_v[:, batch, :], scalar1=1.0)
-                nc.vector.tensor_scalar(
-                    out=odd[:, batch, :], in0=sum_s[:, batch, :],
-                    scalar1=-WORDS * WORD_BIAS, scalar2=1.0 / ODD, op0=ADD, op1=MULT,
-                )
+            if c < SUMMED_EARLY:
+                for t in range(V_ROWS if c < EARLY else 0, PACK):
+                    sum_by_words(h_rows, c, t)
+            if is_outer(c):
+                h_grouped = keep.tile([P, EDGES, PACK], BF16, name="h%d" % c)
+                nc.vector.tensor_copy(out=by_column(h_grouped, all_cols), in_=by_row(h_rows, all_cols))
+                h_tiles.append(h_grouped)
+            else:
+                h_tiles.append(h_rows)
+            done = slice(c // BATCH * BATCH - BATCH, c // BATCH * BATCH)
+            if done.start >= 0 and done.stop <= EARLY:
+                if c % BATCH == 0:
+                    degrees(done, V_ROWS)
+                if c % BATCH == 1:
+                    roots(done)
+                if c % BATCH == 2:
+                    inverses(done)
+                    split_a(done)
+                if c % BATCH == 3:
+                    turn_a(done)
+                if c % BATCH == 4:
+                    keep_a(done)
+            if 4 <= c < 4 + TILES:
+                i = c - 4
                 nc.vector.scalar_tensor_tensor(
-                    out=both[:, batch, :], in0=odd[:, batch, :], scalar=1.0 - ODD, in1=sum_s[:, batch, :],
+                    out=rest[:, i, :], in0=br_ps[:], scalar=gate[:, 0:1], in1=x1_rows[:, i, :],
                     op0=MULT, op1=ADD,
                 )
-                nc.vector.tensor_scalar(
-                    out=deg_v[:, batch, 2:4], in0=both[:, batch, :],
-                    scalar1=-WORDS * WORD_BIAS, scalar2=1.0, op0=ADD, op1=MAX,
-                )
-                nc.scalar.activation(out=root_v[:, batch, :], in_=deg_v[:, batch, :], func=ACT.Sqrt)
-                nc.vector.reciprocal(out=a[:, batch, :], in_=root_v[:, batch, :])
-                ready = [i for i in range(len(outer_passes)) if c + 1 - A_BATCH <= outer_passes[i] <= c]
-                if ready:
-                    some = slice(ready[0], ready[-1] + 1)
-                    a_outer = a[:, batch, :].rearrange("p (n two) t -> p n two t", two=2)[:, :, 1, :]
-                    split_parts(nc, work, "left_a", a_parts[:, some, :], a_outer, 0)
-                    a_ps = psum.tile([P, len(ready), P], BF16, name="a_ps", tag="table", bufs=3)
-                    for i in ready:
-                        nc.tensor.transpose(a_ps[:, i - ready[0], :], a_parts[:, i, :], ident_bf[:])
-                    nc.scalar.copy(out=a_rows[:, some, :], in_=a_ps[:])
 
-        deg_e = keep.tile([P, TILES], F32)
         root_e = keep.tile([P, TILES], F32)
+        floor_e = keep.tile([P, TILES], F32)
         b_col = keep.tile([P, TILES], F32)
         for j in range(TILES):
-            nc.vector.tensor_scalar_max(out=deg_e[:, j : j + 1], in0=col_ps[j][:, 0:1], scalar1=1.0)
-        nc.scalar.activation(out=root_e[:], in_=deg_e[:], func=ACT.Sqrt)
-        nc.vector.reciprocal(out=b_col[:], in_=root_e[:])
+            nc.scalar.activation(out=root_e[:, j : j + 1], in_=col_ps[j][:], func=ACT.Sqrt)
+        nc.vector.tensor_scalar_max(out=floor_e[:], in0=root_e[:], scalar1=1.0)
+        nc.vector.reciprocal(out=b_col[:], in_=floor_e[:])
         b_ps = psum.tile([P, EDGES], F32, tag="spread")
         for j in range(TILES):
-            nc.tensor.matmul(
-                out=b_ps[:, j * P : (j + 1) * P],
-                lhsT=b_col[:, j : j + 1].to_broadcast([P, P]),
-                rhs=ident[:],
-                start=True,
-                stop=True,
+            nc.tensor.transpose(
+                b_ps[:, j * P : (j + 1) * P], b_col[:, j : j + 1].to_broadcast([P, P]), ident[:]
             )
 
         ret_ps = [psum.tile([P, EDGES], F32, name="ret%d" % j, tag="acc%d" % j) for j in range(TILES)]
@@ -245,15 +259,16 @@ def tile_hypergraphgpslayer_pb_k_kernel(
         x_rows_of = {}
         grouped_of = {}
         tables_of = {}
-        order = second_sweep_order()
         x_queue = list(order)
-        table_queue = [c for c in order if is_outer(c)]
+        late_queue = list(range(SUMMED_EARLY, PASSES))
 
-        def fetch_x(c):
-            x_rows_of[c] = work.tile([P, PACK, DIM], BF16, name="x_rows", tag="x_rows", bufs=X_AHEAD)
-            nc.sync.dma_start(out=x_rows_of[c][:], in_=x_view[:, c])
+        def fetch_x():
+            if x_queue:
+                c = x_queue.pop(0)
+                x_rows_of[c] = work.tile([P, PACK, DIM], BF16, name="x_rows", tag="rows", bufs=ROWS_AHEAD)
+                nc.sync.dma_start(out=x_rows_of[c][:], in_=x_view[:, c])
 
-        def spread_b():
+        def spread_b_parts():
             b_wide = b_col[:].unsqueeze(2).to_broadcast([P, TILES, PACK])
             split_parts(nc, work, "left_b", b_parts[:], b_wide, 1)
             parts_ps = psum.tile([P, EDGES], F32, name="parts_ps", tag="table", bufs=3)
@@ -262,6 +277,9 @@ def tile_hypergraphgpslayer_pb_k_kernel(
                     out=parts_ps[:, j * P : (j + 1) * P], lhsT=b_parts[:, j, :], rhs=ident_bf[:],
                     start=True, stop=True,
                 )
+            return parts_ps
+
+        def spread_b(parts_ps):
             nc.vector.tensor_tensor(
                 out=b_rows[:], in0=parts_ps[:].unsqueeze(2).to_broadcast([P, EDGES, PACK]),
                 in1=pick[:].unsqueeze(1).to_broadcast([P, EDGES, PACK]), op=MULT,
@@ -287,12 +305,12 @@ def tile_hypergraphgpslayer_pb_k_kernel(
             on_gpsimd = slice(0, cut)
             on_scalar = slice(cut, DIM)
             nc.gpsimd.tensor_scalar(
-                out=plain_column(x_grouped, on_gpsimd), in0=plain_row(x_rows_of[c], on_gpsimd),
+                out=x_grouped[:, on_gpsimd, :],
+                in0=x_rows_of[c][:, :, on_gpsimd].rearrange("p t c -> p c t"),
                 scalar1=1.0, scalar2=0.0, op0=MULT, op1=ADD,
             )
             nc.scalar.copy(out=by_column(x_grouped, on_scalar), in_=by_row(x_rows_of[c], on_scalar))
-            if x_queue:
-                fetch_x(x_queue.pop(0))
+            fetch_x()
 
         def normalise_h(c):
             if is_outer(c):
@@ -329,54 +347,90 @@ def tile_hypergraphgpslayer_pb_k_kernel(
                     start=first, stop=last,
                 )
 
-        with tc.manual_schedule():
-            for n in range(X_AHEAD):
-                fetch_x(x_queue.pop(0))
-            regroup_x(order[0])
-            normalise_h(order[0])
-            regroup_x(order[1])
-            for n in range(1, PASSES):
-                c = order[n]
-                normalise_h(c)
-                if n == 1:
-                    spread_b()
-                if (n == 1 or is_outer(c)) and table_queue:
-                    make_table(table_queue.pop(0))
-                multiply(order[n - 1], first=(n == 1), last=False)
-                if n + 1 < PASSES:
-                    regroup_x(order[n + 1])
-            multiply(order[-1], first=False, last=True)
+        def sum_late():
+            c = late_queue.pop(0)
+            for t in range(PACK):
+                sum_by_words(h_tiles[c], c, t)
+            return slice(c + 1 - LATE_BATCH, c + 1) if (c + 1) % LATE_BATCH == 0 else None
 
-            r_rows = work.tile([P, PACK, EDGES], BF16, tag="h_norm")
+        w_grouped = keep.tile([P, DIM, PACK], BF16, align_bytes=64)
+
+        def fetch_w():
+            w_rows = work.tile([P, PACK, DIM], BF16, name="w_rows", tag="rows", bufs=ROWS_AHEAD)
+            nc.sync.dma_start(out=w_rows[:], in_=Wr.rearrange("(t p) n -> p t n", p=P))
+            return w_rows
+
+        for n in range(X_AHEAD):
+            fetch_x()
+        regroup_x(order[0])
+        normalise_h(order[0])
+        parts_ps = spread_b_parts()
+        regroup_x(order[1])
+        to_root, to_invert = slice(EARLY, SUMMED_EARLY), None
+        for n in range(1, PASSES):
+            outer = is_outer(order[n])
+            if to_invert:
+                inverses(to_invert)
+            to_invert = to_root
+            if to_root:
+                degrees(to_root, 0)
+                to_root = None
+            normalise_h(order[n])
+            if n == 1:
+                spread_b(parts_ps)
+            if n + 2 < PASSES and is_outer(order[n + 2]):
+                make_table(order[n + 2])
+            multiply(order[n - 1], first=(n == 1), last=False)
+            if n + 1 < PASSES:
+                regroup_x(order[n + 1])
+            if to_invert:
+                roots(to_invert)
+            if outer and late_queue:
+                to_root = sum_late()
+            if n == W_AT - 6:
+                w_rows = fetch_w()
+            if n == W_AT:
+                nc.scalar.copy(out=by_column(w_grouped, all_cols), in_=by_row(w_rows, all_cols))
+        nc.vector.quantize_mx(
+            out=w_codes[:].bitcast(FP8X4), scales=w_scales[:],
+            in_=w_grouped[:].rearrange("p w t -> p (w t)"),
+        )
+        multiply(order[-1], first=False, last=True)
+
+        r_rows = work.tile([P, PACK, EDGES], BF16, tag="h_norm")
+        r_grouped = work.tile([P, EDGES, PACK], BF16, tag="grouped", align_bytes=64)
+        r_codes = work.tile([P, EDGES], U32, tag="codes", align_bytes=64)
+        r_scales = work.tile([P, EDGES], U8, tag="scales", align_bytes=64)
+        halves = [slice(0, EDGES // 2), slice(EDGES // 2, EDGES)]
+        for half in halves:
             for j in range(TILES):
                 if j % 2 == 0:
-                    nc.vector.tensor_copy(out=r_rows[:, j, :], in_=ret_ps[j][:])
+                    nc.vector.tensor_copy(out=r_rows[:, j, half], in_=ret_ps[j][:, half])
                 else:
-                    nc.scalar.copy(out=r_rows[:, j, :], in_=ret_ps[j][:])
-            r_grouped = work.tile([P, EDGES, PACK], BF16, tag="grouped", align_bytes=64)
-            on_vector = slice(0, R_COLS_ON_VECTOR)
-            on_scalar = slice(R_COLS_ON_VECTOR, EDGES)
+                    nc.scalar.copy(out=r_rows[:, j, half], in_=ret_ps[j][:, half])
+        for half in halves:
+            on_vector = slice(half.start, half.start + R_COLS_ON_VECTOR)
+            on_scalar = slice(half.start + R_COLS_ON_VECTOR, half.stop)
             nc.vector.tensor_copy(out=by_column(r_grouped, on_vector), in_=by_row(r_rows, on_vector))
             nc.scalar.copy(out=by_column(r_grouped, on_scalar), in_=by_row(r_rows, on_scalar))
-            r_codes = work.tile([P, EDGES], U32, tag="codes", align_bytes=64)
-            r_scales = work.tile([P, EDGES], U8, tag="scales", align_bytes=64)
+        for half in halves:
             nc.vector.quantize_mx(
-                out=r_codes[:].bitcast(FP8X4), scales=r_scales[:],
-                in_=r_grouped[:].rearrange("p w t -> p (w t)"),
+                out=r_codes[:, half].bitcast(FP8X4), scales=r_scales[:, half],
+                in_=r_grouped[:, half, :].rearrange("p w t -> p (w t)"),
             )
 
-            result = work.tile([P, TILES, DIM], F32, tag="grouped", align_bytes=64)
-            for i in range(TILES):
-                cols = slice(i * P, (i + 1) * P)
-                upd_ps = psum.tile([P, DIM], F32, name="upd%d" % i, tag="acc%d" % i)
-                nc.tensor.matmul_mx(
-                    out=upd_ps[:],
-                    lhsT=r_codes[:, cols].bitcast(FP8X4), lhsT_scale=r_scales[:, cols],
-                    rhs=w_codes[:].bitcast(FP8X4), rhs_scale=w_scales[:],
-                    start=True, stop=True,
-                )
-                nc.vector.scalar_tensor_tensor(
-                    out=result[:, i, :], in0=upd_ps[:], scalar=gate[:, 0:1], in1=rest[:, i, :],
-                    op0=MULT, op1=ADD,
-                )
-                nc.sync.dma_start(out=out[cols, :], in_=result[:, i, :])
+        result = work.tile([P, TILES, DIM], F32, tag="grouped", align_bytes=64)
+        for i in range(TILES):
+            cols = slice(i * P, (i + 1) * P)
+            upd_ps = psum.tile([P, DIM], F32, name="upd%d" % i, tag="acc%d" % i)
+            nc.tensor.matmul_mx(
+                out=upd_ps[:],
+                lhsT=r_codes[:, cols].bitcast(FP8X4), lhsT_scale=r_scales[:, cols],
+                rhs=w_codes[:].bitcast(FP8X4), rhs_scale=w_scales[:],
+                start=True, stop=True,
+            )
+            nc.vector.scalar_tensor_tensor(
+                out=result[:, i, :], in0=upd_ps[:], scalar=gate[:, 0:1], in1=rest[:, i, :],
+                op0=MULT, op1=ADD,
+            )
+            nc.sync.dma_start(out=out[cols, :], in_=result[:, i, :])

@@ -12,7 +12,6 @@ FP8X4 = mybir.dt.float8_e4m3fn_x4
 MULT = mybir.AluOpType.mult
 ADD = mybir.AluOpType.add
 MAX = mybir.AluOpType.max
-X = mybir.AxisListType.X
 ACT = mybir.ActivationFunctionType
 
 NODES, EDGES, DIM = 16384, 512, 512
@@ -22,25 +21,19 @@ K_PASS = P * PACK
 PASSES = NODES // K_PASS
 TILES = 4
 BATCH = 8
-EARLY = 24
-SUMMED_EARLY = 28
-LATE_BATCH = 4
+SUMMED_EARLY = 30
 RUN = 4
-X_COLS_BESIDE_DIRECT = 320
-X_COLS_BESIDE_OUTER = 160
+X_COLS_ON_GPSIMD = 320
 R_COLS_ON_VECTOR = 160
 ROWS_AHEAD = 6
 W_AT = 15
 X_AHEAD = 4
 
-PARTS = 3
-TERMS = [(0, 0), (0, 1), (0, 2), (1, 0), (1, 1), (2, 0)]
-
 WORD_UNIT = 16256.0
 WORD_BIAS = -16384.0
 WORDS = EDGES // 2
 ODD = 65536.0
-V_ROWS = 1
+V_ROWS = 2
 
 FLOPS = 2 * NODES * EDGES * DIM + 2 * EDGES * DIM * DIM
 
@@ -53,35 +46,6 @@ def by_row(rows, cols):
     return rows[:, :, cols].rearrange("p t (c i) -> p c t i", i=RUN)
 
 
-def is_outer(c):
-    return c < EARLY and c % 2 == 1
-
-
-def second_sweep_order():
-    direct = [c for c in range(PASSES) if not is_outer(c)]
-    outer = [c for c in range(PASSES) if is_outer(c)]
-    order = []
-    for g in range(PASSES // 8):
-        d = direct[5 * g : 5 * g + 5]
-        o = outer[3 * g : 3 * g + 3]
-        order += [d[0], d[1], d[2], o[0], d[3], o[1], d[4], o[2]]
-    return order
-
-
-def split_parts(nc, pool, tag, wide, value, terms_index):
-    rest = value
-    n = value.shape[1]
-    for part in range(PARTS):
-        columns = [k for k in range(len(TERMS)) if TERMS[k][terms_index] == part]
-        for k in columns:
-            nc.vector.tensor_copy(out=wide[:, :, PACK * k : PACK * k + PACK], in_=rest)
-        if part + 1 < PARTS:
-            k = columns[0]
-            left = pool.tile([P, n, PACK], F32, name="left", tag=tag)
-            nc.vector.tensor_sub(out=left[:], in0=rest, in1=wide[:, :, PACK * k : PACK * k + PACK])
-            rest = left[:]
-
-
 def tile_hypergraphgpslayer_pb_k_kernel(
     tc, x_0_local, x_1_new, incidence_1, Wr, br, gate_return, out
 ):
@@ -89,8 +53,6 @@ def tile_hypergraphgpslayer_pb_k_kernel(
     h_view = incidence_1.rearrange("(c p t) e -> p c t e", p=P, t=PACK)
     x_view = x_0_local.rearrange("(c p t) d -> p c t d", p=P, t=PACK)
     all_cols = slice(0, 512)
-    order = second_sweep_order()
-    outer_passes = [c for c in range(PASSES) if is_outer(c)]
 
     with ExitStack() as stack:
         keep = stack.enter_context(tc.tile_pool(name="keep", bufs=1))
@@ -108,28 +70,16 @@ def tile_hypergraphgpslayer_pb_k_kernel(
         nc.vector.memset(ones[:], 1.0)
         ident = keep.tile([P, P], F32)
         make_identity(nc, ident[:])
-        a_parts = keep.tile([P, len(outer_passes), P], BF16)
-        nc.gpsimd.memset(a_parts[:], 0.0)
-        b_parts = keep.tile([P, TILES, P], BF16)
-        nc.gpsimd.memset(b_parts[:], 0.0)
-        a_rows = keep.tile([P, len(outer_passes), P], BF16)
-        b_rows = keep.tile([P, EDGES, PACK], BF16)
-        ident_bf = keep.tile([P, P], BF16)
-        nc.vector.tensor_copy(out=ident_bf[:], in_=ident[:])
-        pick = keep.tile([P, PACK], F32)
-        nc.vector.tensor_reduce(
-            out=pick[:], in_=ident[:].rearrange("p (m t) -> p t m", t=PACK), axis=X, op=ADD
-        )
         gate = keep.tile([P, 1], F32)
         nc.scalar.activation(out=gate[:], in_=gate_raw[:], func=ACT.Tanh)
 
-        br_ps = psum.tile([P, DIM], F32, tag="table", bufs=3)
+        br_ps = psum.tile([P, DIM], F32, tag="bias")
         nc.tensor.matmul(out=br_ps[:], lhsT=ones[:], rhs=br_row[:], start=True, stop=True)
         rest = keep.tile([P, TILES, DIM], F32)
         w_codes = keep.tile([P, DIM], U32, align_bytes=64)
         w_scales = keep.tile([P, DIM], U8, align_bytes=64)
 
-        sum_v = keep.tile([P, EARLY, V_ROWS], F32)
+        sum_v = keep.tile([P, PASSES, V_ROWS], F32)
         sum_s = keep.tile([P, PASSES, PACK], F32)
         odd = keep.tile([P, PASSES, PACK], I32)
         both = keep.tile([P, PASSES, PACK], I32)
@@ -138,7 +88,6 @@ def tile_hypergraphgpslayer_pb_k_kernel(
         a = keep.tile([P, PASSES, PACK], F32)
         col_ps = [psum.tile([P, 1], F32, name="col%d" % j, tag="acc%d" % j) for j in range(TILES)]
         h_tiles = []
-        turned = {}
 
         def sum_by_words(h_rows, c, t):
             unread = work.tile([P, WORDS], BF16, name="unread", tag="unread_s")
@@ -172,26 +121,9 @@ def tile_hypergraphgpslayer_pb_k_kernel(
         def inverses(batch):
             nc.vector.reciprocal(out=a[:, batch, :], in_=root_v[:, batch, :])
 
-        def split_a(batch):
-            some = slice(batch.start // 2, batch.stop // 2)
-            a_outer = a[:, batch, :].rearrange("p (n two) t -> p n two t", two=2)[:, :, 1, :]
-            split_parts(nc, work, "left_a", a_parts[:, some, :], a_outer, 0)
-
-        def turn_a(batch):
-            a_ps = psum.tile([P, BATCH // 2, P], BF16, name="a_ps", tag="table", bufs=3)
-            for i in range(BATCH // 2):
-                nc.tensor.transpose(a_ps[:, i, :], a_parts[:, batch.start // 2 + i, :], ident_bf[:])
-            turned[batch.start] = a_ps
-
-        def keep_a(batch):
-            some = slice(batch.start // 2, batch.stop // 2)
-            nc.scalar.copy(out=a_rows[:, some, :], in_=turned[batch.start][:])
-
         for c in range(PASSES):
-            if is_outer(c):
-                h_rows = work.tile([P, PACK, EDGES], BF16, name="h_rows", tag="rows", bufs=ROWS_AHEAD)
-            else:
-                h_rows = keep.tile([P, PACK, EDGES], BF16, name="h%d" % c)
+            h_rows = keep.tile([P, PACK, EDGES], BF16, name="h%d" % c)
+            h_tiles.append(h_rows)
             nc.sync.dma_start(out=h_rows[:], in_=h_view[:, c])
             if c == 3:
                 x1_rows = work.tile([P, TILES, DIM], BF16, tag="rows", bufs=ROWS_AHEAD)
@@ -205,35 +137,23 @@ def tile_hypergraphgpslayer_pb_k_kernel(
                         start=(c == 0 and t == 0),
                         stop=(c == PASSES - 1 and t == PACK - 1),
                     )
-            if c < EARLY:
+            if c < SUMMED_EARLY:
                 for t in range(V_ROWS):
                     unread_v = work.tile([P, EDGES], BF16, tag="unread_v")
                     nc.vector.tensor_scalar(
                         out=unread_v[:], in0=h_rows[:, t, :], scalar1=1.0, scalar2=None,
                         op0=MULT, op1=ADD, accum_out=sum_v[:, c, t : t + 1],
                     )
-            if c < SUMMED_EARLY:
-                for t in range(V_ROWS if c < EARLY else 0, PACK):
+                for t in range(V_ROWS, PACK):
                     sum_by_words(h_rows, c, t)
-            if is_outer(c):
-                h_grouped = keep.tile([P, EDGES, PACK], BF16, name="h%d" % c)
-                nc.vector.tensor_copy(out=by_column(h_grouped, all_cols), in_=by_row(h_rows, all_cols))
-                h_tiles.append(h_grouped)
-            else:
-                h_tiles.append(h_rows)
             done = slice(c // BATCH * BATCH - BATCH, c // BATCH * BATCH)
-            if done.start >= 0 and done.stop <= EARLY:
+            if done.start >= 0:
                 if c % BATCH == 0:
                     degrees(done, V_ROWS)
                 if c % BATCH == 1:
                     roots(done)
                 if c % BATCH == 2:
                     inverses(done)
-                    split_a(done)
-                if c % BATCH == 3:
-                    turn_a(done)
-                if c % BATCH == 4:
-                    keep_a(done)
             if 4 <= c < 4 + TILES:
                 i = c - 4
                 nc.vector.scalar_tensor_tensor(
@@ -258,9 +178,7 @@ def tile_hypergraphgpslayer_pb_k_kernel(
         OF_H, OF_X = 0, 1
         x_rows_of = {}
         grouped_of = {}
-        tables_of = {}
-        x_queue = list(order)
-        late_queue = list(range(SUMMED_EARLY, PASSES))
+        x_queue = list(range(PASSES))
 
         def fetch_x():
             if x_queue:
@@ -268,42 +186,11 @@ def tile_hypergraphgpslayer_pb_k_kernel(
                 x_rows_of[c] = work.tile([P, PACK, DIM], BF16, name="x_rows", tag="rows", bufs=ROWS_AHEAD)
                 nc.sync.dma_start(out=x_rows_of[c][:], in_=x_view[:, c])
 
-        def spread_b_parts():
-            b_wide = b_col[:].unsqueeze(2).to_broadcast([P, TILES, PACK])
-            split_parts(nc, work, "left_b", b_parts[:], b_wide, 1)
-            parts_ps = psum.tile([P, EDGES], F32, name="parts_ps", tag="table", bufs=3)
-            for j in range(TILES):
-                nc.tensor.matmul(
-                    out=parts_ps[:, j * P : (j + 1) * P], lhsT=b_parts[:, j, :], rhs=ident_bf[:],
-                    start=True, stop=True,
-                )
-            return parts_ps
-
-        def spread_b(parts_ps):
-            nc.vector.tensor_tensor(
-                out=b_rows[:], in0=parts_ps[:].unsqueeze(2).to_broadcast([P, EDGES, PACK]),
-                in1=pick[:].unsqueeze(1).to_broadcast([P, EDGES, PACK]), op=MULT,
-            )
-
-        def make_table(c):
-            i = outer_passes.index(c)
-            tables_of[c] = []
-            for half in range(2):
-                table = psum.tile([P, 2, P, PACK], BF16, name="table", tag="table", bufs=3)
-                for q in range(2):
-                    edges = slice((2 * half + q) * P, (2 * half + q + 1) * P)
-                    nc.tensor.matmul(
-                        out=table[:, q].rearrange("p e t -> p (e t)"), lhsT=a_rows[:, i, :],
-                        rhs=b_rows[:, edges, :].rearrange("p e t -> p (e t)"), start=True, stop=True,
-                    )
-                tables_of[c].append(table)
-
         def regroup_x(c):
             grouped_of[c] = work.tile([P, 2, 512, PACK], BF16, name="grouped", tag="grouped", align_bytes=64)
             x_grouped = grouped_of[c][:, OF_X]
-            cut = X_COLS_BESIDE_OUTER if is_outer(c) else X_COLS_BESIDE_DIRECT
-            on_gpsimd = slice(0, cut)
-            on_scalar = slice(cut, DIM)
+            on_gpsimd = slice(0, X_COLS_ON_GPSIMD)
+            on_scalar = slice(X_COLS_ON_GPSIMD, DIM)
             nc.gpsimd.tensor_scalar(
                 out=x_grouped[:, on_gpsimd, :],
                 in0=x_rows_of[c][:, :, on_gpsimd].rearrange("p t c -> p c t"),
@@ -313,15 +200,6 @@ def tile_hypergraphgpslayer_pb_k_kernel(
             fetch_x()
 
         def normalise_h(c):
-            if is_outer(c):
-                for half in range(2):
-                    edges = slice(half * 2 * P, (half + 1) * 2 * P)
-                    nc.vector.tensor_tensor(
-                        out=grouped_of[c][:, OF_H, edges, :].rearrange("p e t -> p (e t)"),
-                        in0=h_tiles[c][:, edges, :].rearrange("p e t -> p (e t)"),
-                        in1=tables_of[c][half][:].rearrange("p q e t -> p (q e t)"), op=MULT,
-                    )
-                return
             h_norm = work.tile([P, PACK, EDGES], BF16, tag="h_norm")
             for t in range(PACK):
                 nc.vector.scalar_tensor_tensor(
@@ -347,12 +225,6 @@ def tile_hypergraphgpslayer_pb_k_kernel(
                     start=first, stop=last,
                 )
 
-        def sum_late():
-            c = late_queue.pop(0)
-            for t in range(PACK):
-                sum_by_words(h_tiles[c], c, t)
-            return slice(c + 1 - LATE_BATCH, c + 1) if (c + 1) % LATE_BATCH == 0 else None
-
         w_grouped = keep.tile([P, DIM, PACK], BF16, align_bytes=64)
 
         def fetch_w():
@@ -362,40 +234,34 @@ def tile_hypergraphgpslayer_pb_k_kernel(
 
         for n in range(X_AHEAD):
             fetch_x()
-        regroup_x(order[0])
-        normalise_h(order[0])
-        parts_ps = spread_b_parts()
-        regroup_x(order[1])
-        to_root, to_invert = slice(EARLY, SUMMED_EARLY), None
-        for n in range(1, PASSES):
-            outer = is_outer(order[n])
-            if to_invert:
-                inverses(to_invert)
-            to_invert = to_root
-            if to_root:
-                degrees(to_root, 0)
-                to_root = None
-            normalise_h(order[n])
-            if n == 1:
-                spread_b(parts_ps)
-            if n + 2 < PASSES and is_outer(order[n + 2]):
-                make_table(order[n + 2])
-            multiply(order[n - 1], first=(n == 1), last=False)
-            if n + 1 < PASSES:
-                regroup_x(order[n + 1])
-            if to_invert:
-                roots(to_invert)
-            if outer and late_queue:
-                to_root = sum_late()
-            if n == W_AT - 6:
+        for c in range(SUMMED_EARLY, PASSES):
+            for t in range(PACK):
+                sum_by_words(h_tiles[c], c, t)
+        last_batch = slice(PASSES - BATCH, PASSES)
+        regroup_x(0)
+        normalise_h(0)
+        regroup_x(1)
+        for c in range(1, PASSES):
+            if c == 1:
+                degrees(slice(last_batch.start, SUMMED_EARLY), V_ROWS)
+                degrees(slice(SUMMED_EARLY, PASSES), 0)
+            if c == 3:
+                inverses(last_batch)
+            normalise_h(c)
+            multiply(c - 1, first=(c == 1), last=False)
+            if c + 1 < PASSES:
+                regroup_x(c + 1)
+            if c == 1:
+                roots(last_batch)
+            if c == W_AT - 6:
                 w_rows = fetch_w()
-            if n == W_AT:
+            if c == W_AT:
                 nc.scalar.copy(out=by_column(w_grouped, all_cols), in_=by_row(w_rows, all_cols))
         nc.vector.quantize_mx(
             out=w_codes[:].bitcast(FP8X4), scales=w_scales[:],
             in_=w_grouped[:].rearrange("p w t -> p (w t)"),
         )
-        multiply(order[-1], first=False, last=True)
+        multiply(PASSES - 1, first=False, last=True)
 
         r_rows = work.tile([P, PACK, EDGES], BF16, tag="h_norm")
         r_grouped = work.tile([P, EDGES, PACK], BF16, tag="grouped", align_bytes=64)

@@ -24,6 +24,7 @@ BATCH = 8
 SUMMED_EARLY = 30
 RUN = 4
 X_COLS_ON_GPSIMD = 320
+LAST_H_COLS_ON_VECTOR = 128
 R_COLS_ON_VECTOR = 160
 ROWS_AHEAD = 6
 W_AT = 15
@@ -60,21 +61,16 @@ def tile_hypergraphgpslayer_pb_k_kernel(
         psum = stack.enter_context(tc.psum_pool(name="psum", bufs=1))
         stack.enter_context(tc.manual_schedule())
 
-        gate_raw = keep.tile([P, 1], BF16)
-        nc.sync.dma_start(out=gate_raw[:], in_=gate_return.partition_broadcast(P))
+        gate_row = keep.tile([P, 16], BF16)
+        nc.vector.memset(gate_row[:], 0.0)
         br_row = keep.tile([P, DIM], BF16)
         nc.vector.memset(br_row[:], 0.0)
-        nc.sync.dma_start(out=br_row[0:1, :], in_=br.rearrange("(o d) -> o d", o=1))
-
+        gate = keep.tile([P, 1], F32)
+        gated_br = keep.tile([P, DIM], F32)
         ones = keep.tile([P, P], BF16)
         nc.vector.memset(ones[:], 1.0)
         ident = keep.tile([P, P], F32)
         make_identity(nc, ident[:])
-        gate = keep.tile([P, 1], F32)
-        nc.scalar.activation(out=gate[:], in_=gate_raw[:], func=ACT.Tanh)
-
-        br_ps = psum.tile([P, DIM], F32, tag="bias")
-        nc.tensor.matmul(out=br_ps[:], lhsT=ones[:], rhs=br_row[:], start=True, stop=True)
         rest = keep.tile([P, TILES, DIM], F32)
         w_codes = keep.tile([P, DIM], U32, align_bytes=64)
         w_scales = keep.tile([P, DIM], U8, align_bytes=64)
@@ -125,9 +121,9 @@ def tile_hypergraphgpslayer_pb_k_kernel(
             h_rows = keep.tile([P, PACK, EDGES], BF16, name="h%d" % c)
             h_tiles.append(h_rows)
             nc.sync.dma_start(out=h_rows[:], in_=h_view[:, c])
-            if c == 3:
-                x1_rows = work.tile([P, TILES, DIM], BF16, tag="rows", bufs=ROWS_AHEAD)
-                nc.sync.dma_start(out=x1_rows[:], in_=x_1_new.rearrange("(i p) d -> p i d", p=P))
+            if c == 1:
+                nc.sync.dma_start(out=gate_row[0:1, 0:1], in_=gate_return.rearrange("(o d) -> o d", o=1))
+                nc.sync.dma_start(out=br_row[0:1, :], in_=br.rearrange("(o d) -> o d", o=1))
             for t in range(PACK):
                 for j in range(TILES):
                     nc.tensor.matmul(
@@ -154,12 +150,15 @@ def tile_hypergraphgpslayer_pb_k_kernel(
                     roots(done)
                 if c % BATCH == 2:
                     inverses(done)
-            if 4 <= c < 4 + TILES:
-                i = c - 4
-                nc.vector.scalar_tensor_tensor(
-                    out=rest[:, i, :], in0=br_ps[:], scalar=gate[:, 0:1], in1=x1_rows[:, i, :],
-                    op0=MULT, op1=ADD,
-                )
+            if c == 3:
+                gate_ps = psum.tile([P, 16], F32, tag="gate")
+                nc.tensor.matmul(out=gate_ps[:], lhsT=ones[:], rhs=gate_row[:], start=True, stop=True)
+                br_ps = psum.tile([P, DIM], F32, tag="bias")
+                nc.tensor.matmul(out=br_ps[:], lhsT=ones[:], rhs=br_row[:], start=True, stop=True)
+            if c == 4:
+                nc.scalar.activation(out=gate[:], in_=gate_ps[:, 0:1], func=ACT.Tanh)
+            if c == 5:
+                nc.scalar.activation(out=gated_br[:], in_=br_ps[:], func=ACT.Copy, scale=gate[:, 0:1])
 
         root_e = keep.tile([P, TILES], F32)
         floor_e = keep.tile([P, TILES], F32)
@@ -178,6 +177,7 @@ def tile_hypergraphgpslayer_pb_k_kernel(
         OF_H, OF_X = 0, 1
         x_rows_of = {}
         grouped_of = {}
+        h_norm_of = {}
         x_queue = list(range(PASSES))
 
         def fetch_x():
@@ -206,7 +206,10 @@ def tile_hypergraphgpslayer_pb_k_kernel(
                     out=h_norm[:, t, :], in0=h_tiles[c][:, t, :],
                     scalar=a[:, c, t : t + 1], in1=b_ps[:], op0=MULT, op1=MULT,
                 )
-            nc.scalar.copy(out=by_column(grouped_of[c][:, OF_H], all_cols), in_=by_row(h_norm, all_cols))
+            h_norm_of[c] = h_norm
+            cut = LAST_H_COLS_ON_VECTOR if c == PASSES - 1 else 0
+            on_scalar = slice(cut, EDGES)
+            nc.scalar.copy(out=by_column(grouped_of[c][:, OF_H], on_scalar), in_=by_row(h_norm, on_scalar))
 
         def multiply(c, first, last):
             codes = work.tile([P, 2, 512], U32, tag="codes", align_bytes=64)
@@ -226,6 +229,14 @@ def tile_hypergraphgpslayer_pb_k_kernel(
                 )
 
         w_grouped = keep.tile([P, DIM, PACK], BF16, align_bytes=64)
+
+        def add_rest(i):
+            nc.gpsimd.tensor_tensor(out=rest[:, i, :], in0=x1_rows[:, i, :], in1=gated_br[:], op=ADD)
+
+        def fetch_x1():
+            x1_rows = keep.tile([P, TILES, DIM], BF16)
+            nc.sync.dma_start(out=x1_rows[:], in_=x_1_new.rearrange("(i p) d -> p i d", p=P))
+            return x1_rows
 
         def fetch_w():
             w_rows = work.tile([P, PACK, DIM], BF16, name="w_rows", tag="rows", bufs=ROWS_AHEAD)
@@ -247,19 +258,29 @@ def tile_hypergraphgpslayer_pb_k_kernel(
                 degrees(slice(SUMMED_EARLY, PASSES), 0)
             if c == 3:
                 inverses(last_batch)
+            if c == W_AT + 4:
+                nc.vector.quantize_mx(
+                    out=w_codes[:].bitcast(FP8X4), scales=w_scales[:],
+                    in_=w_grouped[:].rearrange("p w t -> p (w t)"),
+                )
             normalise_h(c)
             multiply(c - 1, first=(c == 1), last=False)
             if c + 1 < PASSES:
                 regroup_x(c + 1)
+            else:
+                for i in range(TILES):
+                    add_rest(i)
             if c == 1:
                 roots(last_batch)
             if c == W_AT - 6:
                 w_rows = fetch_w()
+                x1_rows = fetch_x1()
             if c == W_AT:
                 nc.scalar.copy(out=by_column(w_grouped, all_cols), in_=by_row(w_rows, all_cols))
-        nc.vector.quantize_mx(
-            out=w_codes[:].bitcast(FP8X4), scales=w_scales[:],
-            in_=w_grouped[:].rearrange("p w t -> p (w t)"),
+        last = PASSES - 1
+        on_vector = slice(0, LAST_H_COLS_ON_VECTOR)
+        nc.vector.tensor_copy(
+            out=by_column(grouped_of[last][:, OF_H], on_vector), in_=by_row(h_norm_of[last], on_vector)
         )
         multiply(PASSES - 1, first=False, last=True)
 

from contextlib import ExitStack

import concourse.mybir as mybir
from concourse.masks import make_identity

BF16 = mybir.dt.bfloat16
F32 = mybir.dt.float32
U32 = mybir.dt.uint32
U8 = mybir.dt.uint8
I32 = mybir.dt.int32
FP8X4 = mybir.dt.float8_e4m3fn_x4
MULT = mybir.AluOpType.mult
ADD = mybir.AluOpType.add
MAX = mybir.AluOpType.max
ACT = mybir.ActivationFunctionType

NODES, EDGES, DIM = 16384, 512, 512
P = 128
PACK = 4
K_PASS = P * PACK
PASSES = NODES // K_PASS
TILES = 4
BATCH = 8
SUMMED_EARLY = 30
RUN = 4
X_COLS_ON_GPSIMD = 320
LAST_H_COLS_ON_VECTOR = 128
R_COLS_ON_VECTOR = 160
ROWS_AHEAD = 6
W_AT = 15
X_AHEAD = 4

WORD_UNIT = 16256.0
WORD_BIAS = -16384.0
WORDS = EDGES // 2
ODD = 65536.0
V_ROWS = 2

FLOPS = 2 * NODES * EDGES * DIM + 2 * EDGES * DIM * DIM


def by_column(grouped, cols):
    return grouped[:, cols, :].rearrange("p (c i) t -> p c t i", i=RUN)


def by_row(rows, cols):
    return rows[:, :, cols].rearrange("p t (c i) -> p c t i", i=RUN)


def tile_hypergraphgpslayer_pb_k_kernel(
    tc, x_0_local, x_1_new, incidence_1, Wr, br, gate_return, out
):
    nc = tc.nc
    h_view = incidence_1.rearrange("(c p t) e -> p c t e", p=P, t=PACK)
    x_view = x_0_local.rearrange("(c p t) d -> p c t d", p=P, t=PACK)
    all_cols = slice(0, 512)

    with ExitStack() as stack:
        keep = stack.enter_context(tc.tile_pool(name="keep", bufs=1))
        work = stack.enter_context(tc.tile_pool(name="work", bufs=2))
        psum = stack.enter_context(tc.psum_pool(name="psum", bufs=1))
        stack.enter_context(tc.manual_schedule())

        gate_row = keep.tile([P, 16], BF16)
        nc.vector.memset(gate_row[:], 0.0)
        br_row = keep.tile([P, DIM], BF16)
        nc.vector.memset(br_row[:], 0.0)
        gate = keep.tile([P, 1], F32)
        gated_br = keep.tile([P, DIM], F32)
        ones = keep.tile([P, P], BF16)
        nc.vector.memset(ones[:], 1.0)
        ident = keep.tile([P, P], F32)
        make_identity(nc, ident[:])
        rest = keep.tile([P, TILES, DIM], F32)
        w_codes = keep.tile([P, DIM], U32, align_bytes=64)
        w_scales = keep.tile([P, DIM], U8, align_bytes=64)

        sum_v = keep.tile([P, PASSES, V_ROWS], F32)
        sum_s = keep.tile([P, PASSES, PACK], F32)
        odd = keep.tile([P, PASSES, PACK], I32)
        both = keep.tile([P, PASSES, PACK], I32)
        deg_v = keep.tile([P, PASSES, PACK], F32)
        root_v = keep.tile([P, PASSES, PACK], F32)
        a = keep.tile([P, PASSES, PACK], F32)
        col_ps = [psum.tile([P, 1], F32, name="col%d" % j, tag="acc%d" % j) for j in range(TILES)]
        h_tiles = []

        def sum_by_words(h_rows, c, t):
            unread = work.tile([P, WORDS], BF16, name="unread", tag="unread_s")
            nc.scalar.activation(
                out=unread[:], in_=h_rows[:, t, :].bitcast(U32), func=ACT.Copy,
                scale=1.0 / WORD_UNIT, bias=WORD_BIAS, accum_out=sum_s[:, c, t : t + 1],
            )

        def degrees(batch, first_word_row):
            if first_word_row:
                nc.vector.tensor_scalar_max(
                    out=deg_v[:, batch, 0:first_word_row], in0=sum_v[:, batch, :], scalar1=1.0
                )
            rows = slice(first_word_row, PACK)
            nc.vector.tensor_scalar(
                out=odd[:, batch, rows], in0=sum_s[:, batch, rows],
                scalar1=-WORDS * WORD_BIAS, scalar2=1.0 / ODD, op0=ADD, op1=MULT,
            )
            nc.vector.scalar_tensor_tensor(
                out=both[:, batch, rows], in0=odd[:, batch, rows], scalar=1.0 - ODD,
                in1=sum_s[:, batch, rows], op0=MULT, op1=ADD,
            )
            nc.vector.tensor_scalar(
                out=deg_v[:, batch, rows], in0=both[:, batch, rows],
                scalar1=-WORDS * WORD_BIAS, scalar2=1.0, op0=ADD, op1=MAX,
            )

        def roots(batch):
            nc.scalar.activation(out=root_v[:, batch, :], in_=deg_v[:, batch, :], func=ACT.Sqrt)

        def inverses(batch):
            nc.vector.reciprocal(out=a[:, batch, :], in_=root_v[:, batch, :])

        for c in range(PASSES):
            h_rows = keep.tile([P, PACK, EDGES], BF16, name="h%d" % c)
            h_tiles.append(h_rows)
            nc.sync.dma_start(out=h_rows[:], in_=h_view[:, c])
            if c == 1:
                nc.sync.dma_start(out=gate_row[0:1, 0:1], in_=gate_return.rearrange("(o d) -> o d", o=1))
                nc.sync.dma_start(out=br_row[0:1, :], in_=br.rearrange("(o d) -> o d", o=1))
            for t in range(PACK):
                for j in range(TILES):
                    nc.tensor.matmul(
                        out=col_ps[j][:],
                        lhsT=h_rows[:, t, j * P : (j + 1) * P],
                        rhs=ones[:, :1],
                        start=(c == 0 and t == 0),
                        stop=(c == PASSES - 1 and t == PACK - 1),
                    )
            if c < SUMMED_EARLY:
                for t in range(V_ROWS):
                    unread_v = work.tile([P, EDGES], BF16, tag="unread_v")
                    nc.vector.tensor_scalar(
                        out=unread_v[:], in0=h_rows[:, t, :], scalar1=1.0, scalar2=None,
                        op0=MULT, op1=ADD, accum_out=sum_v[:, c, t : t + 1],
                    )
                for t in range(V_ROWS, PACK):
                    sum_by_words(h_rows, c, t)
            done = slice(c // BATCH * BATCH - BATCH, c // BATCH * BATCH)
            if done.start >= 0:
                if c % BATCH == 0:
                    degrees(done, V_ROWS)
                if c % BATCH == 1:
                    roots(done)
                if c % BATCH == 2:
                    inverses(done)
            if c == 3:
                gate_ps = psum.tile([P, 16], F32, tag="gate")
                nc.tensor.matmul(out=gate_ps[:], lhsT=ones[:], rhs=gate_row[:], start=True, stop=True)
                br_ps = psum.tile([P, DIM], F32, tag="bias")
                nc.tensor.matmul(out=br_ps[:], lhsT=ones[:], rhs=br_row[:], start=True, stop=True)
            if c == 4:
                nc.scalar.activation(out=gate[:], in_=gate_ps[:, 0:1], func=ACT.Tanh)
            if c == 5:
                nc.scalar.activation(out=gated_br[:], in_=br_ps[:], func=ACT.Copy, scale=gate[:, 0:1])

        root_e = keep.tile([P, TILES], F32)
        floor_e = keep.tile([P, TILES], F32)
        b_col = keep.tile([P, TILES], F32)
        for j in range(TILES):
            nc.scalar.activation(out=root_e[:, j : j + 1], in_=col_ps[j][:], func=ACT.Sqrt)
        nc.vector.tensor_scalar_max(out=floor_e[:], in0=root_e[:], scalar1=1.0)
        nc.vector.reciprocal(out=b_col[:], in_=floor_e[:])
        b_ps = psum.tile([P, EDGES], F32, tag="spread")
        for j in range(TILES):
            nc.tensor.transpose(
                b_ps[:, j * P : (j + 1) * P], b_col[:, j : j + 1].to_broadcast([P, P]), ident[:]
            )

        ret_ps = [psum.tile([P, EDGES], F32, name="ret%d" % j, tag="acc%d" % j) for j in range(TILES)]
        OF_H, OF_X = 0, 1
        x_rows_of = {}
        grouped_of = {}
        h_norm_of = {}
        x_queue = list(range(PASSES))

        def fetch_x():
            if x_queue:
                c = x_queue.pop(0)
                x_rows_of[c] = work.tile([P, PACK, DIM], BF16, name="x_rows", tag="rows", bufs=ROWS_AHEAD)
                nc.sync.dma_start(out=x_rows_of[c][:], in_=x_view[:, c])

        def regroup_x(c):
            grouped_of[c] = work.tile([P, 2, 512, PACK], BF16, name="grouped", tag="grouped", align_bytes=64)
            x_grouped = grouped_of[c][:, OF_X]
            on_gpsimd = slice(0, X_COLS_ON_GPSIMD)
            on_scalar = slice(X_COLS_ON_GPSIMD, DIM)
            nc.gpsimd.tensor_scalar(
                out=x_grouped[:, on_gpsimd, :],
                in0=x_rows_of[c][:, :, on_gpsimd].rearrange("p t c -> p c t"),
                scalar1=1.0, scalar2=0.0, op0=MULT, op1=ADD,
            )
            nc.scalar.copy(out=by_column(x_grouped, on_scalar), in_=by_row(x_rows_of[c], on_scalar))
            fetch_x()

        def normalise_h(c):
            h_norm = work.tile([P, PACK, EDGES], BF16, tag="h_norm")
            for t in range(PACK):
                nc.vector.scalar_tensor_tensor(
                    out=h_norm[:, t, :], in0=h_tiles[c][:, t, :],
                    scalar=a[:, c, t : t + 1], in1=b_ps[:], op0=MULT, op1=MULT,
                )
            h_norm_of[c] = h_norm
            cut = LAST_H_COLS_ON_VECTOR if c == PASSES - 1 else 0
            on_scalar = slice(cut, EDGES)
            nc.scalar.copy(out=by_column(grouped_of[c][:, OF_H], on_scalar), in_=by_row(h_norm, on_scalar))

        def multiply(c, first, last):
            codes = work.tile([P, 2, 512], U32, tag="codes", align_bytes=64)
            scales = work.tile([P, 2, 512], U8, tag="scales", align_bytes=64)
            nc.vector.quantize_mx(
                out=codes[:].rearrange("p o w -> p (o w)").bitcast(FP8X4),
                scales=scales[:].rearrange("p o w -> p (o w)"),
                in_=grouped_of[c][:].rearrange("p o w t -> p (o w t)"),
            )
            for j in range(TILES):
                cols = slice(j * P, (j + 1) * P)
                nc.tensor.matmul_mx(
                    out=ret_ps[j][:],
                    lhsT=codes[:, OF_X, cols].bitcast(FP8X4), lhsT_scale=scales[:, OF_X, cols],
                    rhs=codes[:, OF_H, :].bitcast(FP8X4), rhs_scale=scales[:, OF_H, :],
                    start=first, stop=last,
                )

        w_grouped = keep.tile([P, DIM, PACK], BF16, align_bytes=64)

        def add_rest(i):
            nc.gpsimd.tensor_tensor(out=rest[:, i, :], in0=x1_rows[:, i, :], in1=gated_br[:], op=ADD)

        def fetch_x1():
            x1_rows = keep.tile([P, TILES, DIM], BF16)
            nc.sync.dma_start(out=x1_rows[:], in_=x_1_new.rearrange("(i p) d -> p i d", p=P))
            return x1_rows

        def fetch_w():
            w_rows = work.tile([P, PACK, DIM], BF16, name="w_rows", tag="rows", bufs=ROWS_AHEAD)
            nc.sync.dma_start(out=w_rows[:], in_=Wr.rearrange("(t p) n -> p t n", p=P))
            return w_rows

        for n in range(X_AHEAD):
            fetch_x()
        for c in range(SUMMED_EARLY, PASSES):
            for t in range(PACK):
                sum_by_words(h_tiles[c], c, t)
        last_batch = slice(PASSES - BATCH, PASSES)
        regroup_x(0)
        normalise_h(0)
        regroup_x(1)
        for c in range(1, PASSES):
            if c == 1:
                degrees(slice(last_batch.start, SUMMED_EARLY), V_ROWS)
                degrees(slice(SUMMED_EARLY, PASSES), 0)
            if c == 3:
                inverses(last_batch)
            if c == W_AT + 4:
                nc.vector.quantize_mx(
                    out=w_codes[:].bitcast(FP8X4), scales=w_scales[:],
                    in_=w_grouped[:].rearrange("p w t -> p (w t)"),
                )
            normalise_h(c)
            multiply(c - 1, first=(c == 1), last=False)
            if c + 1 < PASSES:
                regroup_x(c + 1)
            else:
                for i in range(TILES):
                    add_rest(i)
            if c == 1:
                roots(last_batch)
            if c == W_AT - 6:
                w_rows = fetch_w()
                x1_rows = fetch_x1()
            if c == W_AT:
                nc.scalar.copy(out=by_column(w_grouped, all_cols), in_=by_row(w_rows, all_cols))
        last = PASSES - 1
        on_vector = slice(0, LAST_H_COLS_ON_VECTOR)
        nc.vector.tensor_copy(
            out=by_column(grouped_of[last][:, OF_H], on_vector), in_=by_row(h_norm_of[last], on_vector)
        )
        multiply(PASSES - 1, first=False, last=True)

        r_rows = work.tile([P, PACK, EDGES], BF16, tag="h_norm")
        r_grouped = work.tile([P, EDGES, PACK], BF16, tag="grouped", align_bytes=64)
        r_codes = work.tile([P, EDGES], U32, tag="codes", align_bytes=64)
        r_scales = work.tile([P, EDGES], U8, tag="scales", align_bytes=64)
        halves = [slice(0, EDGES // 2), slice(EDGES // 2, EDGES)]
        for half in halves:
            for j in range(TILES):
                if j % 2 == 0:
                    nc.vector.tensor_copy(out=r_rows[:, j, half], in_=ret_ps[j][:, half])
                else:
                    nc.scalar.copy(out=r_rows[:, j, half], in_=ret_ps[j][:, half])
        for half in halves:
            on_vector = slice(half.start, half.start + R_COLS_ON_VECTOR)
            on_scalar = slice(half.start + R_COLS_ON_VECTOR, half.stop)
            nc.vector.tensor_copy(out=by_column(r_grouped, on_vector), in_=by_row(r_rows, on_vector))
            nc.scalar.copy(out=by_column(r_grouped, on_scalar), in_=by_row(r_rows, on_scalar))
        for half in halves:
            nc.vector.quantize_mx(
                out=r_codes[:, half].bitcast(FP8X4), scales=r_scales[:, half],
                in_=r_grouped[:, half, :].rearrange("p w t -> p (w t)"),
            )

        result = work.tile([P, TILES, DIM], F32, tag="grouped", align_bytes=64)
        for i in range(TILES):
            cols = slice(i * P, (i + 1) * P)
            upd_ps = psum.tile([P, DIM], F32, name="upd%d" % i, tag="acc%d" % i)
            nc.tensor.matmul_mx(
                out=upd_ps[:],
                lhsT=r_codes[:, cols].bitcast(FP8X4), lhsT_scale=r_scales[:, cols],
                rhs=w_codes[:].bitcast(FP8X4), rhs_scale=w_scales[:],
                start=True, stop=True,
            )
            nc.vector.scalar_tensor_tensor(
                out=result[:, i, :], in0=upd_ps[:], scalar=gate[:, 0:1], in1=rest[:, i, :],
                op0=MULT, op1=ADD,
            )
            nc.sync.dma_start(out=out[cols, :], in_=result[:, i, :])
